import numpy as np
import ml_dtypes


def mxq(x, axis, fmt="e4m3"):
    dtype, down = {"e4m3": (ml_dtypes.float8_e4m3fn, 7), "e5m2": (ml_dtypes.float8_e5m2, 14)}[fmt]
    v = np.moveaxis(np.asarray(x, np.float32).astype(ml_dtypes.bfloat16).astype(np.float64), axis, -1)
    blocks = v.reshape(v.shape[:-1] + (-1, 32))
    amax = np.abs(blocks).max(-1, keepdims=True)
    byte = np.maximum(np.where(amax > 0, np.frexp(amax)[1] - 1 + 127, 0) - down, 1)
    scale = np.exp2(byte - 127.0)
    codes = (blocks / scale).astype(np.float32).astype(dtype).astype(np.float64)
    return np.moveaxis((codes * scale).reshape(v.shape), -1, axis)


WIDE = False


def mx_kscale(k):
    if not WIDE:
        return np.ones(k)
    levels = np.array([10, -10, 5, -5, 0])
    a = np.random.permutation(np.resize(levels, k // 512 * 4)).reshape(k // 512, 4)
    idx = np.arange(k)
    return np.exp2(a[idx // 512, idx % 128 // 32])


BF16 = ml_dtypes.bfloat16


def bf(x):
    return np.asarray(x, np.float32).astype(BF16)


def f64(x):
    return np.asarray(x).astype(np.float64)


N, RES = 1024, 1024
SIGMA = 0.02


def setup_inputs():
    s = mx_kscale(N)
    r = np.minimum(s, 1.0) ** 2
    d = np.sqrt(np.log(1.0 / r) * 2.0 * SIGMA * SIGMA)
    pos = np.random.random_sample((N, 2))
    act = np.random.standard_normal(N)
    scale = bf(0.9 + 0.03 * np.random.standard_normal(1))
    sc = float(f64(scale)[0])
    pos[:, 0] = np.where(r < 1.0, 0.5 + (-d - 0.5) / sc, pos[:, 0])
    return {"positions": bf(pos),
            "activities": bf(act / r),
            "position_scale": scale}


def reference(positions, activities, position_scale):
    positions, activities, position_scale = f64(positions), f64(activities), f64(position_scale)
    grid = np.linspace(0.0, 1.0, RES)
    inv_two_sigma_sq = 1.0 / (2.0 * SIGMA * SIGMA)
    ps = 0.5 + position_scale * (positions - 0.5)
    x = ps[:, 0]
    y = 1.0 - ps[:, 1]
    gx = np.exp(-(grid[None, :] - x[:, None]) ** 2 * inv_two_sigma_sq)
    gy = np.exp(-(grid[None, :] - y[:, None]) ** 2 * inv_two_sigma_sq)
    return mxq(gy * activities[:, None], 0, "e4m3").T @ mxq(gx, 0, "e4m3")

@@ -1,0 +1,227 @@
+import math
+from contextlib import ExitStack
+
+import concourse.mybir as mybir
+
+F32 = mybir.dt.float32
+BF16 = mybir.dt.bfloat16
+I32 = mybir.dt.int32
+U32 = mybir.dt.uint32
+U8 = mybir.dt.uint8
+FP8X4 = mybir.dt.float8_e4m3fn_x4
+ACT = mybir.ActivationFunctionType
+ALU = mybir.AluOpType
+
+P = 128
+PACK = 4
+RES = 1024
+NPTS = 1024
+PASSES = NPTS // (P * PACK)
+NCT = PASSES * PACK
+NG = 2 * NCT
+WH = 64
+NCLS = 2
+WF = WH * NCLS
+NM = RES // WF
+C_PIX = 1250.0 / (1023.0 * 1023.0)
+MAGIC = 12582912.0
+SHIFT = 0.125
+FLOPS = 2 * RES * RES * NPTS
+
+
+def tile_gaussiansplatting_t_kernel(tc, positions, activities, position_scale, out):
+    nc = tc.nc
+    with ExitStack() as ctx:
+        const = ctx.enter_context(tc.tile_pool(name="const", bufs=1))
+        keep = ctx.enter_context(tc.tile_pool(name="keep", bufs=1))
+        wpool = ctx.enter_context(tc.tile_pool(name="wpool", bufs=2))
+        epool = ctx.enter_context(tc.tile_pool(name="epool", bufs=4))
+        gpool = ctx.enter_context(tc.tile_pool(name="gpool", bufs=3))
+        opool = ctx.enter_context(tc.tile_pool(name="opool", bufs=6))
+        psum = ctx.enter_context(tc.psum_pool(name="psum", bufs=8))
+        ctx.enter_context(tc.manual_schedule())
+
+        pos_sb = const.tile([P, PASSES, PACK * 2], BF16)
+        nc.sync.dma_start(out=pos_sb[:], in_=positions.rearrange("(c p t) d -> p c (t d)", c=PASSES, p=P, t=PACK))
+        scl_sb = const.tile([P, 1], BF16)
+        nc.scalar.dma_start(out=scl_sb[:], in_=position_scale.partition_broadcast(P))
+        act_sb = const.tile([P, PASSES, PACK], BF16)
+        nc.sync.dma_start(out=act_sb[:], in_=activities.rearrange("(c p t) -> p c t", c=PASSES, p=P, t=PACK))
+
+        j_int = const.tile([P, WH], I32)
+        nc.gpsimd.iota(j_int[:], pattern=[[1, WH]], base=0, channel_multiplier=0)
+        j_off = const.tile([P, WH], F32)
+        nc.vector.tensor_scalar(out=j_off[:], in0=j_int[:], scalar1=-(WH - 1) / 2.0, scalar2=None, op0=ALU.add)
+        frame0 = const.tile([P, NM], F32)
+        nc.vector.tensor_scalar(out=frame0[:], in0=j_int[:, 0:NM], scalar1=float(WF), scalar2=None, op0=ALU.mult)
+        sign2 = const.tile([P, 2], F32)
+        nc.vector.memset(sign2[:, 0:1], 1.0)
+        nc.vector.memset(sign2[:, 1:2], -1.0)
+        rtab = const.tile([P, NCLS], F32)
+        for e in range(NCLS):
+            nc.vector.memset(rtab[:, e:e + 1], (511.5 - (e * WH + (WH - 1) / 2.0)) / WF + MAGIC)
+
+        s2 = const.tile([P, 2], F32)
+        nc.vector.tensor_scalar(out=s2[:], in0=sign2[:], scalar1=scl_sb[:, 0:1], scalar2=None, op0=ALU.mult)
+        qs = const.tile([P, 2, NCT], F32)
+        nc.vector.scalar_tensor_tensor(
+            out=qs[:].rearrange("p k g -> p g k"), in0=pos_sb[:].rearrange("p c (t d) -> p (c t) d", d=2), scalar=-0.5,
+            in1=s2[:].unsqueeze(1).to_broadcast([P, NCT, 2]), op0=ALU.add, op1=ALU.mult,
+        )
+        qf = qs[:].rearrange("p k g -> p (k g)")
+        qf_e = qf.unsqueeze(1).to_broadcast([P, NCLS, NG])
+        rnd = const.tile([P, NCLS, NG], F32)
+        nc.vector.scalar_tensor_tensor(
+            out=rnd[:], in0=qf_e, scalar=1023.0 / WF, in1=rtab[:].unsqueeze(2).to_broadcast([P, NCLS, NG]),
+            op0=ALU.mult, op1=ALU.add,
+        )
+        q1024 = const.tile([P, NG], F32)
+        nc.vector.tensor_scalar(out=q1024[:], in0=qf, scalar1=-1024.0, scalar2=None, op0=ALU.mult)
+        low = const.tile([P, NCLS, NG], F32)
+        nc.vector.tensor_scalar(out=low[:], in0=rnd[:], scalar1=-MAGIC, scalar2=0.0, op0=ALU.add, op1=ALU.max)
+        home = const.tile([P, NCLS, NG], F32)
+        nc.vector.tensor_scalar(out=home[:], in0=low[:], scalar1=float(NM - 1), scalar2=float(WF), op0=ALU.min, op1=ALU.mult)
+        part = const.tile([P, NCLS, NG], F32)
+        nc.vector.tensor_tensor(out=part[:], in0=home[:], in1=q1024[:].unsqueeze(1).to_broadcast([P, NCLS, NG]), op=ALU.add)
+        dref = const.tile([P, NCLS, NG], F32)
+        for e in range(NCLS):
+            first = e * WH + (WH - 1) / 2.0
+            nc.vector.scalar_tensor_tensor(out=dref[:, e, :], in0=part[:, e, :], scalar=first - 511.5, in1=qf, op0=ALU.add, op1=ALU.add)
+        NEG = NCLS * NG
+        hop = const.tile([P, NM, NEG], F32)
+        nc.vector.tensor_tensor(
+            out=hop[:],
+            in0=frame0[:].unsqueeze(2).to_broadcast([P, NM, NEG]),
+            in1=home[:].rearrange("p e g -> p (e g)").unsqueeze(1).to_broadcast([P, NM, NEG]),
+            op=ALU.subtract,
+        )
+        span = const.tile([P, NM, NEG], F32)
+        nc.vector.scalar_tensor_tensor(
+            out=span[:], in0=dref[:].rearrange("p e g -> p (e g)").unsqueeze(1).to_broadcast([P, NM, NEG]),
+            scalar=2.0, in1=hop[:], op0=ALU.mult, op1=ALU.add,
+        )
+        offs = const.tile([P, NM, NEG], F32)
+        nc.vector.scalar_tensor_tensor(out=offs[:], in0=hop[:], scalar=-C_PIX, in1=span[:], op0=ALU.mult, op1=ALU.mult)
+        slope = const.tile([P, NM, NEG], F32)
+        nc.vector.tensor_scalar(out=slope[:], in0=hop[:], scalar1=-2.0 * C_PIX, scalar2=None, op0=ALU.mult)
+
+        window = const.tile([P, 2, PASSES, WF, PACK], F32)
+
+        def make_window(kind, c):
+            sq = wpool.tile([P, PACK, NCLS, WH], F32, tag="wsq")
+            for t in range(PACK):
+                for e in range(NCLS):
+                    gg = kind * NCT + c * PACK + t
+                    nc.scalar.activation(out=sq[:, t, e, :], in_=j_off[:], func=ACT.Square, bias=dref[:, e, gg:gg + 1], scale=1.0)
+            ea = wpool.tile([P, PACK, WF], F32, tag="wea")
+            nc.scalar.activation(out=ea[:], in_=sq[:].rearrange("p t e w -> p t (e w)"), func=ACT.Exp, scale=-C_PIX)
+            eb = wpool.tile([P, PACK, WF], F32, tag="web")
+            nc.scalar.activation(out=eb[:], in_=sq[:].rearrange("p t e w -> p t (e w)"), func=ACT.Exp, scale=-C_PIX, bias=SHIFT)
+            if kind == 0:
+                nc.vector.scalar_tensor_tensor(
+                    out=window[:, kind, c], in0=eb[:].rearrange("p t w -> p w t"), scalar=math.exp(-SHIFT),
+                    in1=ea[:].rearrange("p t w -> p w t"), op0=ALU.mult, op1=ALU.max,
+                )
+            else:
+                best = wpool.tile([P, PACK, WF], F32, tag="wbest")
+                nc.vector.scalar_tensor_tensor(out=best[:], in0=eb[:], scalar=math.exp(-SHIFT), in1=ea[:], op0=ALU.mult, op1=ALU.max)
+                nc.vector.tensor_tensor(
+                    out=window[:, kind, c], in0=best[:].rearrange("p t w -> p w t"),
+                    in1=act_sb[:, c, :].unsqueeze(1).to_broadcast([P, WF, PACK]), op=ALU.mult,
+                )
+
+        gx_codes = keep.tile([P, PASSES, RES], U32, align_bytes=64)
+        gx_scales = keep.tile([P, PASSES, RES], U8, align_bytes=64)
+        a_codes = keep.tile([P, PASSES, RES], U32, align_bytes=64)
+        a_scales = keep.tile([P, PASSES, RES], U8, align_bytes=64)
+
+        steps = []
+        for col0, ncols in ((0, 256), (256, 256)):
+            steps.extend([(0, c, col0, ncols) for c in range(PASSES)])
+        for col0, ncols in ((0, 256), (256, 256)):
+            steps.extend([(1, c, col0, ncols) for c in range(PASSES)])
+        steps.extend([(0, c, 512, 512) for c in range(PASSES)])
+        for col0, ncols in ((512, 256), (768, 128), (896, 128)):
+            steps.extend([(1, c, col0, ncols) for c in range(PASSES)])
+        windows_before = {0: [(0, 0)], 1: [(0, 1)], 2: [(1, 0)], 3: [(1, 1)]}
+        ready = {7 - 2: [(0, 0), (1, 0)], 7: [(2, 0), (3, 0)], 9: [(0, 1), (1, 1), (2, 1), (3, 1)],
+                 11: [(4, 0), (4, 1), (5, 0), (5, 1)], 13: [(6, 0), (6, 1)], 15: [(7, 0), (7, 1)]}
+        fars = {}
+        groupeds = {}
+        accs = {}
+
+        def far_field(i):
+            kind, c, col0, ncols = steps[i]
+            far = epool.tile([P, PACK, ncols], F32, tag="far", name="far")
+            fars[i] = far
+            for t in range(PACK):
+                g = kind * NCT + c * PACK + t
+                for f in range(ncols // WF):
+                    m = col0 // WF + f
+                    for e in range(NCLS):
+                        idx = e * NG + g
+                        lo = f * WF + e * WH
+                        nc.scalar.activation(
+                            out=far[:, t, lo:lo + WH], in_=j_off[:], func=ACT.Exp,
+                            bias=offs[:, m, idx:idx + 1], scale=slope[:, m, idx:idx + 1],
+                        )
+
+        def multiply(i):
+            kind, c, col0, ncols = steps[i]
+            frames = ncols // WF
+            grouped = gpool.tile([P, ncols, PACK], BF16, tag="grouped", name="grouped", align_bytes=64)
+            groupeds[i] = grouped
+            nc.vector.tensor_tensor(
+                out=grouped[:].rearrange("p (f w) t -> p f w t", f=frames),
+                in0=fars[i][:].rearrange("p t (f w) -> p f w t", f=frames),
+                in1=window[:, kind, c].unsqueeze(1).to_broadcast([P, frames, WF, PACK]),
+                op=ALU.mult,
+            )
+
+        def quantise(i):
+            kind, c, col0, ncols = steps[i]
+            codes, scales = (gx_codes, gx_scales) if kind == 0 else (a_codes, a_scales)
+            cols = slice(col0, col0 + ncols)
+            nc.vector.quantize_mx(
+                out=codes[:, c, cols].bitcast(FP8X4), scales=scales[:, c, cols],
+                in_=groupeds[i][:].rearrange("p w t -> p (w t)"),
+            )
+
+        def product(m, nb):
+            rows = slice(m * P, (m + 1) * P)
+            wcols = slice(nb * 512, (nb + 1) * 512)
+            acc = psum.tile([P, 512], F32, tag="acc", name="acc")
+            accs[(m, nb)] = acc
+            for c in range(PASSES):
+                nc.tensor.matmul_mx(
+                    out=acc[:],
+                    lhsT=a_codes[:, c, rows].bitcast(FP8X4), lhsT_scale=a_scales[:, c, rows],
+                    rhs=gx_codes[:, c, wcols].bitcast(FP8X4), rhs_scale=gx_scales[:, c, wcols],
+                    start=(c == 0), stop=(c == PASSES - 1),
+                )
+
+        counter = [0]
+
+        def leave(m, nb):
+            stage = opool.tile([P, 512], F32, tag="stage", name="stage")
+            if counter[0] in (5, 10, 15):
+                nc.scalar.copy(out=stage[:], in_=accs[(m, nb)][:])
+            else:
+                nc.vector.tensor_copy(out=stage[:], in_=accs[(m, nb)][:])
+            counter[0] += 1
+            nc.sync.dma_start(out=out[m * P:(m + 1) * P, nb * 512:(nb + 1) * 512], in_=stage[:])
+
+        n = len(steps)
+        for i in range(n + 3):
+            for kind, c in windows_before.get(i, []):
+                make_window(kind, c)
+            if i < n:
+                far_field(i)
+            if 0 <= i - 1 < n:
+                multiply(i - 1)
+            if 0 <= i - 2 < n:
+                quantise(i - 2)
+                for m, nb in ready.get(i - 2, []):
+                    product(m, nb)
+            for m, nb in ready.get(i - 3, []):
+                leave(m, nb)

@@ -105,29 +105,29 @@ def tile_gaussiansplatting_t_kernel(tc, positions, activities, position_scale, o
         slope = const.tile([P, NM, NEG], F32)
         nc.vector.tensor_scalar(out=slope[:], in0=hop[:], scalar1=-2.0 * C_PIX, scalar2=None, op0=ALU.mult)
 
-        window = const.tile([P, 2, PASSES, WF, PACK], F32)
+        window = const.tile([P, 2, PASSES, WF // 4, PACK, 4], F32)
+        j_runs = j_off[:].rearrange("p (g i) -> p g i", i=4)
 
         def make_window(kind, c):
-            sq = wpool.tile([P, PACK, NCLS, WH], F32, tag="wsq")
+            sq = wpool.tile([P, WF // 4, PACK, 4], F32, tag="wsq")
             for t in range(PACK):
                 for e in range(NCLS):
                     gg = kind * NCT + c * PACK + t
-                    nc.scalar.activation(out=sq[:, t, e, :], in_=j_off[:], func=ACT.Square, bias=dref[:, e, gg:gg + 1], scale=1.0)
-            ea = wpool.tile([P, PACK, WF], F32, tag="wea")
-            nc.scalar.activation(out=ea[:], in_=sq[:].rearrange("p t e w -> p t (e w)"), func=ACT.Exp, scale=-C_PIX)
-            eb = wpool.tile([P, PACK, WF], F32, tag="web")
-            nc.scalar.activation(out=eb[:], in_=sq[:].rearrange("p t e w -> p t (e w)"), func=ACT.Exp, scale=-C_PIX, bias=SHIFT)
+                    nc.scalar.activation(out=sq[:, e * WH // 4:(e + 1) * WH // 4, t, :], in_=j_runs, func=ACT.Square, bias=dref[:, e, gg:gg + 1], scale=1.0)
+            ea = wpool.tile([P, WF // 4, PACK, 4], F32, tag="wea")
+            nc.scalar.activation(out=ea[:], in_=sq[:], func=ACT.Exp, scale=-C_PIX)
+            eb = wpool.tile([P, WF // 4, PACK, 4], F32, tag="web")
+            nc.scalar.activation(out=eb[:], in_=sq[:], func=ACT.Exp, scale=-C_PIX, bias=SHIFT)
             if kind == 0:
                 nc.vector.scalar_tensor_tensor(
-                    out=window[:, kind, c], in0=eb[:].rearrange("p t w -> p w t"), scalar=math.exp(-SHIFT),
-                    in1=ea[:].rearrange("p t w -> p w t"), op0=ALU.mult, op1=ALU.max,
+                    out=window[:, kind, c], in0=eb[:], scalar=math.exp(-SHIFT), in1=ea[:], op0=ALU.mult, op1=ALU.max,
                 )
             else:
-                best = wpool.tile([P, PACK, WF], F32, tag="wbest")
+                best = wpool.tile([P, WF // 4, PACK, 4], F32, tag="wbest")
                 nc.vector.scalar_tensor_tensor(out=best[:], in0=eb[:], scalar=math.exp(-SHIFT), in1=ea[:], op0=ALU.mult, op1=ALU.max)
                 nc.vector.tensor_tensor(
-                    out=window[:, kind, c], in0=best[:].rearrange("p t w -> p w t"),
-                    in1=act_sb[:, c, :].unsqueeze(1).to_broadcast([P, WF, PACK]), op=ALU.mult,
+                    out=window[:, kind, c], in0=best[:],
+                    in1=act_sb[:, c, :].unsqueeze(1).unsqueeze(3).to_broadcast([P, WF // 4, PACK, 4]), op=ALU.mult,
                 )
 
         gx_codes = keep.tile([P, PASSES, RES], U32, align_bytes=64)
@@ -152,7 +152,7 @@ def tile_gaussiansplatting_t_kernel(tc, positions, activities, position_scale, o
 
         def far_field(i):
             kind, c, col0, ncols = steps[i]
-            far = epool.tile([P, PACK, ncols], F32, tag="far", name="far")
+            far = epool.tile([P, ncols // 4, PACK, 4], F32, tag="far", name="far")
             fars[i] = far
             for t in range(PACK):
                 g = kind * NCT + c * PACK + t
@@ -162,7 +162,7 @@ def tile_gaussiansplatting_t_kernel(tc, positions, activities, position_scale, o
                         idx = e * NG + g
                         lo = f * WF + e * WH
                         nc.scalar.activation(
-                            out=far[:, t, lo:lo + WH], in_=j_off[:], func=ACT.Exp,
+                            out=far[:, lo // 4:(lo + WH) // 4, t, :], in_=j_runs, func=ACT.Exp,
                             bias=offs[:, m, idx:idx + 1], scale=slope[:, m, idx:idx + 1],
                         )
 
@@ -172,9 +172,9 @@ def tile_gaussiansplatting_t_kernel(tc, positions, activities, position_scale, o
             grouped = gpool.tile([P, ncols, PACK], BF16, tag="grouped", name="grouped", align_bytes=64)
             groupeds[i] = grouped
             nc.vector.tensor_tensor(
-                out=grouped[:].rearrange("p (f w) t -> p f w t", f=frames),
-                in0=fars[i][:].rearrange("p t (f w) -> p f w t", f=frames),
-                in1=window[:, kind, c].unsqueeze(1).to_broadcast([P, frames, WF, PACK]),
+                out=grouped[:].rearrange("p (f g i) t -> p f g t i", f=frames, i=4),
+                in0=fars[i][:].rearrange("p (f g) t i -> p f g t i", f=frames),
+                in1=window[:, kind, c].unsqueeze(1).to_broadcast([P, frames, WF // 4, PACK, 4]),
                 op=ALU.mult,
             )
 
@@ -204,7 +204,7 @@ def tile_gaussiansplatting_t_kernel(tc, positions, activities, position_scale, o
 
         def leave(m, nb):
             stage = opool.tile([P, 512], F32, tag="stage", name="stage")
-            if counter[0] in (5, 10, 15):
+            if counter[0] % 2 == 1:
                 nc.scalar.copy(out=stage[:], in_=accs[(m, nb)][:])
             else:
                 nc.vector.tensor_copy(out=stage[:], in_=accs[(m, nb)][:])

@@ -37,9 +37,8 @@ def tile_gaussiansplatting_t_kernel(tc, positions, activities, position_scale, o
         wpool = ctx.enter_context(tc.tile_pool(name="wpool", bufs=2))
         epool = ctx.enter_context(tc.tile_pool(name="epool", bufs=4))
         gpool = ctx.enter_context(tc.tile_pool(name="gpool", bufs=3))
-        opool = ctx.enter_context(tc.tile_pool(name="opool", bufs=6))
+        opool = ctx.enter_context(tc.tile_pool(name="opool", bufs=4))
         psum = ctx.enter_context(tc.psum_pool(name="psum", bufs=8))
-        ctx.enter_context(tc.manual_schedule())
 
         pos_sb = const.tile([P, PASSES, PACK * 2], BF16)
         nc.sync.dma_start(out=pos_sb[:], in_=positions.rearrange("(c p t) d -> p c (t d)", c=PASSES, p=P, t=PACK))
@@ -108,55 +107,39 @@ def tile_gaussiansplatting_t_kernel(tc, positions, activities, position_scale, o
         window = const.tile([P, 2, PASSES, WF // 4, PACK, 4], F32)
         j_runs = j_off[:].rearrange("p (g i) -> p g i", i=4)
 
-        def make_window(kind, c):
-            sq = wpool.tile([P, WF // 4, PACK, 4], F32, tag="wsq")
-            for t in range(PACK):
+        def make_window(kind):
+            sq = wpool.tile([P, PASSES, WF // 4, PACK, 4], F32, tag="wsq")
+            for g in range(NCT):
                 for e in range(NCLS):
-                    gg = kind * NCT + c * PACK + t
-                    nc.scalar.activation(out=sq[:, e * WH // 4:(e + 1) * WH // 4, t, :], in_=j_runs, func=ACT.Square, bias=dref[:, e, gg:gg + 1], scale=1.0)
-            ea = wpool.tile([P, WF // 4, PACK, 4], F32, tag="wea")
+                    gg = kind * NCT + g
+                    nc.scalar.activation(out=sq[:, g // PACK, e * WH // 4:(e + 1) * WH // 4, g % PACK, :], in_=j_runs, func=ACT.Square, bias=dref[:, e, gg:gg + 1], scale=1.0)
+            ea = wpool.tile([P, PASSES, WF // 4, PACK, 4], F32, tag="wea")
             nc.scalar.activation(out=ea[:], in_=sq[:], func=ACT.Exp, scale=-C_PIX)
-            eb = wpool.tile([P, WF // 4, PACK, 4], F32, tag="web")
+            eb = wpool.tile([P, PASSES, WF // 4, PACK, 4], F32, tag="web")
             nc.scalar.activation(out=eb[:], in_=sq[:], func=ACT.Exp, scale=-C_PIX, bias=SHIFT)
             if kind == 0:
-                nc.vector.scalar_tensor_tensor(
-                    out=window[:, kind, c], in0=eb[:], scalar=math.exp(-SHIFT), in1=ea[:], op0=ALU.mult, op1=ALU.max,
-                )
+                nc.vector.scalar_tensor_tensor(out=window[:, kind], in0=eb[:], scalar=math.exp(-SHIFT), in1=ea[:], op0=ALU.mult, op1=ALU.max)
             else:
-                best = wpool.tile([P, WF // 4, PACK, 4], F32, tag="wbest")
+                best = wpool.tile([P, PASSES, WF // 4, PACK, 4], F32, tag="wbest")
                 nc.vector.scalar_tensor_tensor(out=best[:], in0=eb[:], scalar=math.exp(-SHIFT), in1=ea[:], op0=ALU.mult, op1=ALU.max)
-                nc.vector.tensor_tensor(
-                    out=window[:, kind, c], in0=best[:],
-                    in1=act_sb[:, c, :].unsqueeze(1).unsqueeze(3).to_broadcast([P, WF // 4, PACK, 4]), op=ALU.mult,
-                )
+                for c in range(PASSES):
+                    nc.vector.tensor_tensor(
+                        out=window[:, kind, c], in0=best[:, c],
+                        in1=act_sb[:, c, :].unsqueeze(1).unsqueeze(3).to_broadcast([P, WF // 4, PACK, 4]), op=ALU.mult,
+                    )
 
         gx_codes = keep.tile([P, PASSES, RES], U32, align_bytes=64)
         gx_scales = keep.tile([P, PASSES, RES], U8, align_bytes=64)
         a_codes = keep.tile([P, PASSES, RES], U32, align_bytes=64)
         a_scales = keep.tile([P, PASSES, RES], U8, align_bytes=64)
 
-        steps = []
-        for col0, ncols in ((0, 256), (256, 256)):
-            steps.extend([(0, c, col0, ncols) for c in range(PASSES)])
-        for col0, ncols in ((0, 256), (256, 256)):
-            steps.extend([(1, c, col0, ncols) for c in range(PASSES)])
-        steps.extend([(0, c, 512, 512) for c in range(PASSES)])
-        for col0, ncols in ((512, 256), (768, 128), (896, 128)):
-            steps.extend([(1, c, col0, ncols) for c in range(PASSES)])
-        windows_before = {0: [(0, 0)], 1: [(0, 1)], 2: [(1, 0)], 3: [(1, 1)]}
-        ready = {7 - 2: [(0, 0), (1, 0)], 7: [(2, 0), (3, 0)], 9: [(0, 1), (1, 1), (2, 1), (3, 1)],
-                 11: [(4, 0), (4, 1), (5, 0), (5, 1)], 13: [(6, 0), (6, 1)], 15: [(7, 0), (7, 1)]}
-        fars = {}
-        groupeds = {}
-        accs = {}
-
-        def far_field(i):
-            kind, c, col0, ncols = steps[i]
-            far = epool.tile([P, ncols // 4, PACK, 4], F32, tag="far", name="far")
-            fars[i] = far
+        def make(kind, c, col0, ncols):
+            codes, scales = (gx_codes, gx_scales) if kind == 0 else (a_codes, a_scales)
+            frames = ncols // WF
+            far = epool.tile([P, ncols // 4, PACK, 4], F32, tag="far%d" % ncols)
             for t in range(PACK):
                 g = kind * NCT + c * PACK + t
-                for f in range(ncols // WF):
+                for f in range(frames):
                     m = col0 // WF + f
                     for e in range(NCLS):
                         idx = e * NG + g
@@ -165,33 +148,25 @@ def tile_gaussiansplatting_t_kernel(tc, positions, activities, position_scale, o
                             out=far[:, lo // 4:(lo + WH) // 4, t, :], in_=j_runs, func=ACT.Exp,
                             bias=offs[:, m, idx:idx + 1], scale=slope[:, m, idx:idx + 1],
                         )
-
-        def multiply(i):
-            kind, c, col0, ncols = steps[i]
-            frames = ncols // WF
-            grouped = gpool.tile([P, ncols, PACK], BF16, tag="grouped", name="grouped", align_bytes=64)
-            groupeds[i] = grouped
+            grouped = gpool.tile([P, ncols, PACK], BF16, tag="grouped%d" % ncols, align_bytes=64)
             nc.vector.tensor_tensor(
                 out=grouped[:].rearrange("p (f g i) t -> p f g t i", f=frames, i=4),
-                in0=fars[i][:].rearrange("p (f g) t i -> p f g t i", f=frames),
+                in0=far[:].rearrange("p (f g) t i -> p f g t i", f=frames),
                 in1=window[:, kind, c].unsqueeze(1).to_broadcast([P, frames, WF // 4, PACK, 4]),
                 op=ALU.mult,
             )
-
-        def quantise(i):
-            kind, c, col0, ncols = steps[i]
-            codes, scales = (gx_codes, gx_scales) if kind == 0 else (a_codes, a_scales)
             cols = slice(col0, col0 + ncols)
             nc.vector.quantize_mx(
                 out=codes[:, c, cols].bitcast(FP8X4), scales=scales[:, c, cols],
-                in_=groupeds[i][:].rearrange("p w t -> p (w t)"),
+                in_=grouped[:].rearrange("p w t -> p (w t)"),
             )
+
+        stages = {}
 
         def product(m, nb):
             rows = slice(m * P, (m + 1) * P)
             wcols = slice(nb * 512, (nb + 1) * 512)
-            acc = psum.tile([P, 512], F32, tag="acc", name="acc")
-            accs[(m, nb)] = acc
+            acc = psum.tile([P, 512], F32, tag="acc")
             for c in range(PASSES):
                 nc.tensor.matmul_mx(
                     out=acc[:],
@@ -199,29 +174,40 @@ def tile_gaussiansplatting_t_kernel(tc, positions, activities, position_scale, o
                     rhs=gx_codes[:, c, wcols].bitcast(FP8X4), rhs_scale=gx_scales[:, c, wcols],
                     start=(c == 0), stop=(c == PASSES - 1),
                 )
-
-        counter = [0]
-
-        def leave(m, nb):
-            stage = opool.tile([P, 512], F32, tag="stage", name="stage")
-            if counter[0] % 2 == 1:
-                nc.scalar.copy(out=stage[:], in_=accs[(m, nb)][:])
+            stage = opool.tile([P, 512], F32, tag="stage")
+            if (m + nb) % 2 == 0:
+                nc.scalar.copy(out=stage[:], in_=acc[:])
             else:
-                nc.vector.tensor_copy(out=stage[:], in_=accs[(m, nb)][:])
-            counter[0] += 1
-            nc.sync.dma_start(out=out[m * P:(m + 1) * P, nb * 512:(nb + 1) * 512], in_=stage[:])
+                nc.vector.tensor_copy(out=stage[:], in_=acc[:])
+            nc.sync.dma_start(out=out[rows, wcols], in_=stage[:])
 
-        n = len(steps)
-        for i in range(n + 3):
-            for kind, c in windows_before.get(i, []):
-                make_window(kind, c)
-            if i < n:
-                far_field(i)
-            if 0 <= i - 1 < n:
-                multiply(i - 1)
-            if 0 <= i - 2 < n:
-                quantise(i - 2)
-                for m, nb in ready.get(i - 2, []):
-                    product(m, nb)
-            for m, nb in ready.get(i - 3, []):
-                leave(m, nb)
+        def gx_block(nb):
+            for c in range(PASSES):
+                make(0, c, nb * 512, 512)
+
+        def a_block(col0, ncols):
+            for c in range(PASSES):
+                make(1, c, col0, ncols)
+
+        make_window(0)
+        gx_block(0)
+        make_window(1)
+        a_block(0, 256)
+        for m in (0, 1):
+            product(m, 0)
+        a_block(256, 256)
+        for m in (2, 3):
+            product(m, 0)
+        gx_block(1)
+        for m in (0, 1, 2, 3):
+            product(m, 1)
+        a_block(512, 256)
+        for m in (4, 5):
+            product(m, 0)
+            product(m, 1)
+        a_block(768, 128)
+        product(6, 0)
+        product(6, 1)
+        a_block(896, 128)
+        product(7, 0)
+        product(7, 1)

@@ -24,7 +24,7 @@ NCLS = 2
 WF = WH * NCLS
 NM = RES // WF
 C_PIX = 1250.0 / (1023.0 * 1023.0)
-MAGIC = 12582912.0
+MAGIC = 1.5 * 2.0 ** 23 * WF
 SHIFT = 0.125
 FLOPS = 2 * RES * RES * NPTS
 
@@ -58,7 +58,7 @@ def tile_gaussiansplatting_t_kernel(tc, positions, activities, position_scale, o
         nc.vector.memset(sign2[:, 1:2], -1.0)
         rtab = const.tile([P, NCLS], F32)
         for e in range(NCLS):
-            nc.vector.memset(rtab[:, e:e + 1], (511.5 - (e * WH + (WH - 1) / 2.0)) / WF + MAGIC)
+            nc.vector.memset(rtab[:, e:e + 1], 511.5 - (e * WH + (WH - 1) / 2.0))
 
         s2 = const.tile([P, 2], F32)
         nc.vector.tensor_scalar(out=s2[:], in0=sign2[:], scalar1=scl_sb[:, 0:1], scalar2=None, op0=ALU.mult)
@@ -71,15 +71,15 @@ def tile_gaussiansplatting_t_kernel(tc, positions, activities, position_scale, o
         qf_e = qf.unsqueeze(1).to_broadcast([P, NCLS, NG])
         rnd = const.tile([P, NCLS, NG], F32)
         nc.vector.scalar_tensor_tensor(
-            out=rnd[:], in0=qf_e, scalar=1023.0 / WF, in1=rtab[:].unsqueeze(2).to_broadcast([P, NCLS, NG]),
+            out=rnd[:], in0=qf_e, scalar=1023.0, in1=rtab[:].unsqueeze(2).to_broadcast([P, NCLS, NG]),
             op0=ALU.mult, op1=ALU.add,
         )
         q1024 = const.tile([P, NG], F32)
         nc.vector.tensor_scalar(out=q1024[:], in0=qf, scalar1=-1024.0, scalar2=None, op0=ALU.mult)
         low = const.tile([P, NCLS, NG], F32)
-        nc.vector.tensor_scalar(out=low[:], in0=rnd[:], scalar1=-MAGIC, scalar2=0.0, op0=ALU.add, op1=ALU.max)
+        nc.vector.tensor_scalar(out=low[:], in0=rnd[:], scalar1=MAGIC, scalar2=MAGIC, op0=ALU.add, op1=ALU.max)
         home = const.tile([P, NCLS, NG], F32)
-        nc.vector.tensor_scalar(out=home[:], in0=low[:], scalar1=float(NM - 1), scalar2=float(WF), op0=ALU.min, op1=ALU.mult)
+        nc.vector.tensor_scalar(out=home[:], in0=low[:], scalar1=MAGIC + float(WF * (NM - 1)), scalar2=-MAGIC, op0=ALU.min, op1=ALU.add)
         part = const.tile([P, NCLS, NG], F32)
         nc.vector.tensor_tensor(out=part[:], in0=home[:], in1=q1024[:].unsqueeze(1).to_broadcast([P, NCLS, NG]), op=ALU.add)
         dref = const.tile([P, NCLS, NG], F32)

@@ -34,7 +34,7 @@ def tile_gaussiansplatting_t_kernel(tc, positions, activities, position_scale, o
     with ExitStack() as ctx:
         const = ctx.enter_context(tc.tile_pool(name="const", bufs=1))
         keep = ctx.enter_context(tc.tile_pool(name="keep", bufs=1))
-        wpool = ctx.enter_context(tc.tile_pool(name="wpool", bufs=2))
+        wpool = ctx.enter_context(tc.tile_pool(name="wpool", bufs=4))
         epool = ctx.enter_context(tc.tile_pool(name="epool", bufs=4))
         gpool = ctx.enter_context(tc.tile_pool(name="gpool", bufs=3))
         opool = ctx.enter_context(tc.tile_pool(name="opool", bufs=4))
@@ -56,10 +56,26 @@ def tile_gaussiansplatting_t_kernel(tc, positions, activities, position_scale, o
         sign2 = const.tile([P, 2], F32)
         nc.vector.memset(sign2[:, 0:1], 1.0)
         nc.vector.memset(sign2[:, 1:2], -1.0)
+        sign1023 = const.tile([P, 2], F32)
+        nc.vector.memset(sign1023[:, 0:1], 1023.0)
+        nc.vector.memset(sign1023[:, 1:2], -1023.0)
         rtab = const.tile([P, NCLS], F32)
         for e in range(NCLS):
             nc.vector.memset(rtab[:, e:e + 1], 511.5 - (e * WH + (WH - 1) / 2.0))
 
+        pos_v = pos_sb[:].rearrange("p c (t d) -> p (c t) d", d=2)
+        rough = const.tile([P, 2, NCT], F32)
+        nc.vector.scalar_tensor_tensor(
+            out=rough[:].rearrange("p k g -> p g k"), in0=pos_v, scalar=-0.5,
+            in1=sign1023[:].unsqueeze(1).to_broadcast([P, NCT, 2]), op0=ALU.add, op1=ALU.mult,
+        )
+        rnd = const.tile([P, NCLS, NG], F32)
+        nc.vector.scalar_tensor_tensor(
+            out=rnd[:], in0=rough[:].rearrange("p k g -> p (k g)").unsqueeze(1).to_broadcast([P, NCLS, NG]), scalar=scl_sb[:, 0:1],
+            in1=rtab[:].unsqueeze(2).to_broadcast([P, NCLS, NG]), op0=ALU.mult, op1=ALU.add,
+        )
+        low = const.tile([P, NCLS, NG], F32)
+        nc.vector.tensor_scalar(out=low[:], in0=rnd[:], scalar1=MAGIC, scalar2=MAGIC, op0=ALU.add, op1=ALU.max)
         s2 = const.tile([P, 2], F32)
         nc.vector.tensor_scalar(out=s2[:], in0=sign2[:], scalar1=scl_sb[:, 0:1], scalar2=None, op0=ALU.mult)
         qs = const.tile([P, 2, NCT], F32)
@@ -68,16 +84,8 @@ def tile_gaussiansplatting_t_kernel(tc, positions, activities, position_scale, o
             in1=s2[:].unsqueeze(1).to_broadcast([P, NCT, 2]), op0=ALU.add, op1=ALU.mult,
         )
         qf = qs[:].rearrange("p k g -> p (k g)")
-        qf_e = qf.unsqueeze(1).to_broadcast([P, NCLS, NG])
-        rnd = const.tile([P, NCLS, NG], F32)
-        nc.vector.scalar_tensor_tensor(
-            out=rnd[:], in0=qf_e, scalar=1023.0, in1=rtab[:].unsqueeze(2).to_broadcast([P, NCLS, NG]),
-            op0=ALU.mult, op1=ALU.add,
-        )
         q1024 = const.tile([P, NG], F32)
         nc.vector.tensor_scalar(out=q1024[:], in0=qf, scalar1=-1024.0, scalar2=None, op0=ALU.mult)
-        low = const.tile([P, NCLS, NG], F32)
-        nc.vector.tensor_scalar(out=low[:], in0=rnd[:], scalar1=MAGIC, scalar2=MAGIC, op0=ALU.add, op1=ALU.max)
         home = const.tile([P, NCLS, NG], F32)
         nc.vector.tensor_scalar(out=home[:], in0=low[:], scalar1=MAGIC + float(WF * (NM - 1)), scalar2=-MAGIC, op0=ALU.min, op1=ALU.add)
         part = const.tile([P, NCLS, NG], F32)
@@ -107,26 +115,29 @@ def tile_gaussiansplatting_t_kernel(tc, positions, activities, position_scale, o
         window = const.tile([P, 2, PASSES, WF // 4, PACK, 4], F32)
         j_runs = j_off[:].rearrange("p (g i) -> p g i", i=4)
 
-        def make_window(kind):
-            sq = wpool.tile([P, PASSES, WF // 4, PACK, 4], F32, tag="wsq")
-            for g in range(NCT):
+        def make_window(kind, c):
+            dist = wpool.tile([P, WF // 4, PACK, 4], F32, tag="wdist")
+            for t in range(PACK):
                 for e in range(NCLS):
-                    gg = kind * NCT + g
-                    nc.scalar.activation(out=sq[:, g // PACK, e * WH // 4:(e + 1) * WH // 4, g % PACK, :], in_=j_runs, func=ACT.Square, bias=dref[:, e, gg:gg + 1], scale=1.0)
-            ea = wpool.tile([P, PASSES, WF // 4, PACK, 4], F32, tag="wea")
+                    gg = kind * NCT + c * PACK + t
+                    nc.vector.tensor_scalar(
+                        out=dist[:, e * WH // 4:(e + 1) * WH // 4, t, :], in0=j_runs, scalar1=dref[:, e, gg:gg + 1], scalar2=None, op0=ALU.add,
+                    )
+            sq = wpool.tile([P, WF // 4, PACK, 4], F32, tag="wsq")
+            nc.vector.tensor_tensor(out=sq[:], in0=dist[:], in1=dist[:], op=ALU.mult)
+            ea = wpool.tile([P, WF // 4, PACK, 4], F32, tag="wea")
             nc.scalar.activation(out=ea[:], in_=sq[:], func=ACT.Exp, scale=-C_PIX)
-            eb = wpool.tile([P, PASSES, WF // 4, PACK, 4], F32, tag="web")
+            eb = wpool.tile([P, WF // 4, PACK, 4], F32, tag="web")
             nc.scalar.activation(out=eb[:], in_=sq[:], func=ACT.Exp, scale=-C_PIX, bias=SHIFT)
             if kind == 0:
-                nc.vector.scalar_tensor_tensor(out=window[:, kind], in0=eb[:], scalar=math.exp(-SHIFT), in1=ea[:], op0=ALU.mult, op1=ALU.max)
+                nc.vector.scalar_tensor_tensor(out=window[:, kind, c], in0=eb[:], scalar=math.exp(-SHIFT), in1=ea[:], op0=ALU.mult, op1=ALU.max)
             else:
-                best = wpool.tile([P, PASSES, WF // 4, PACK, 4], F32, tag="wbest")
+                best = wpool.tile([P, WF // 4, PACK, 4], F32, tag="wbest")
                 nc.vector.scalar_tensor_tensor(out=best[:], in0=eb[:], scalar=math.exp(-SHIFT), in1=ea[:], op0=ALU.mult, op1=ALU.max)
-                for c in range(PASSES):
-                    nc.vector.tensor_tensor(
-                        out=window[:, kind, c], in0=best[:, c],
-                        in1=act_sb[:, c, :].unsqueeze(1).unsqueeze(3).to_broadcast([P, WF // 4, PACK, 4]), op=ALU.mult,
-                    )
+                nc.vector.tensor_tensor(
+                    out=window[:, kind, c], in0=best[:],
+                    in1=act_sb[:, c, :].unsqueeze(1).unsqueeze(3).to_broadcast([P, WF // 4, PACK, 4]), op=ALU.mult,
+                )
 
         gx_codes = keep.tile([P, PASSES, RES], U32, align_bytes=64)
         gx_scales = keep.tile([P, PASSES, RES], U8, align_bytes=64)
@@ -175,7 +186,7 @@ def tile_gaussiansplatting_t_kernel(tc, positions, activities, position_scale, o
                     start=(c == 0), stop=(c == PASSES - 1),
                 )
             stage = opool.tile([P, 512], F32, tag="stage")
-            if (m + nb) % 2 == 0:
+            if (2 * m + nb) % 4 != 3:
                 nc.scalar.copy(out=stage[:], in_=acc[:])
             else:
                 nc.vector.tensor_copy(out=stage[:], in_=acc[:])
@@ -189,9 +200,14 @@ def tile_gaussiansplatting_t_kernel(tc, positions, activities, position_scale, o
             for c in range(PASSES):
                 make(1, c, col0, ncols)
 
-        make_window(0)
-        gx_block(0)
-        make_window(1)
+        make_window(0, 0)
+        make(0, 0, 0, 256)
+        make_window(0, 1)
+        make(0, 1, 0, 256)
+        make_window(1, 0)
+        make_window(1, 1)
+        make(0, 0, 256, 256)
+        make(0, 1, 256, 256)
         a_block(0, 256)
         for m in (0, 1):
             product(m, 0)

@@ -37,7 +37,7 @@ def tile_gaussiansplatting_t_kernel(tc, positions, activities, position_scale, o
         wpool = ctx.enter_context(tc.tile_pool(name="wpool", bufs=4))
         epool = ctx.enter_context(tc.tile_pool(name="epool", bufs=4))
         gpool = ctx.enter_context(tc.tile_pool(name="gpool", bufs=3))
-        opool = ctx.enter_context(tc.tile_pool(name="opool", bufs=4))
+        opool = ctx.enter_context(tc.tile_pool(name="opool", bufs=16))
         psum = ctx.enter_context(tc.psum_pool(name="psum", bufs=8))
 
         pos_sb = const.tile([P, PASSES, PACK * 2], BF16)

@@ -102,21 +102,17 @@ def tile_gaussiansplatting_t_kernel(tc, positions, activities, position_scale, o
             in1=home[:].rearrange("p e g -> p (e g)").unsqueeze(1).to_broadcast([P, NM, NEG]),
             op=ALU.subtract,
         )
-        span = const.tile([P, NM, NEG], F32)
-        nc.vector.scalar_tensor_tensor(
-            out=span[:], in0=dref[:].rearrange("p e g -> p (e g)").unsqueeze(1).to_broadcast([P, NM, NEG]),
-            scalar=2.0, in1=hop[:], op0=ALU.mult, op1=ALU.add,
-        )
         offs = const.tile([P, NM, NEG], F32)
-        nc.vector.scalar_tensor_tensor(out=offs[:], in0=hop[:], scalar=-C_PIX, in1=span[:], op0=ALU.mult, op1=ALU.mult)
+        nc.vector.scalar_tensor_tensor(out=offs[:], in0=hop[:], scalar=-C_PIX, in1=hop[:], op0=ALU.mult, op1=ALU.mult)
         slope = const.tile([P, NM, NEG], F32)
         nc.vector.tensor_scalar(out=slope[:], in0=hop[:], scalar1=-2.0 * C_PIX, scalar2=None, op0=ALU.mult)
 
         window = const.tile([P, 2, PASSES, WF // 4, PACK, 4], F32)
         j_runs = j_off[:].rearrange("p (g i) -> p g i", i=4)
+        dists = const.tile([P, 2, PASSES, WF // 4, PACK, 4], F32)
 
         def make_window(kind, c):
-            dist = wpool.tile([P, WF // 4, PACK, 4], F32, tag="wdist")
+            dist = dists[:, kind, c]
             for t in range(PACK):
                 for e in range(NCLS):
                     gg = kind * NCT + c * PACK + t
@@ -124,7 +120,7 @@ def tile_gaussiansplatting_t_kernel(tc, positions, activities, position_scale, o
                         out=dist[:, e * WH // 4:(e + 1) * WH // 4, t, :], in0=j_runs, scalar1=dref[:, e, gg:gg + 1], scalar2=None, op0=ALU.add,
                     )
             sq = wpool.tile([P, WF // 4, PACK, 4], F32, tag="wsq")
-            nc.vector.tensor_tensor(out=sq[:], in0=dist[:], in1=dist[:], op=ALU.mult)
+            nc.vector.tensor_tensor(out=sq[:], in0=dist, in1=dist, op=ALU.mult)
             ea = wpool.tile([P, WF // 4, PACK, 4], F32, tag="wea")
             nc.scalar.activation(out=ea[:], in_=sq[:], func=ACT.Exp, scale=-C_PIX)
             eb = wpool.tile([P, WF // 4, PACK, 4], F32, tag="web")
@@ -156,7 +152,7 @@ def tile_gaussiansplatting_t_kernel(tc, positions, activities, position_scale, o
                         idx = e * NG + g
                         lo = f * WF + e * WH
                         nc.scalar.activation(
-                            out=far[:, lo // 4:(lo + WH) // 4, t, :], in_=j_runs, func=ACT.Exp,
+                            out=far[:, lo // 4:(lo + WH) // 4, t, :], in_=dists[:, kind, c, e * WH // 4:(e + 1) * WH // 4, t, :], func=ACT.Exp,
                             bias=offs[:, m, idx:idx + 1], scale=slope[:, m, idx:idx + 1],
                         )
             grouped = gpool.tile([P, ncols, PACK], BF16, tag="grouped%d" % ncols, align_bytes=64)
@@ -186,7 +182,7 @@ def tile_gaussiansplatting_t_kernel(tc, positions, activities, position_scale, o
                     start=(c == 0), stop=(c == PASSES - 1),
                 )
             stage = opool.tile([P, 512], F32, tag="stage")
-            if (2 * m + nb) % 4 != 3:
+            if (2 * m + nb) % 8 != 7:
                 nc.scalar.copy(out=stage[:], in_=acc[:])
             else:
                 nc.vector.tensor_copy(out=stage[:], in_=acc[:])

@@ -37,7 +37,7 @@ def tile_gaussiansplatting_t_kernel(tc, positions, activities, position_scale, o
         wpool = ctx.enter_context(tc.tile_pool(name="wpool", bufs=4))
         epool = ctx.enter_context(tc.tile_pool(name="epool", bufs=4))
         gpool = ctx.enter_context(tc.tile_pool(name="gpool", bufs=3))
-        opool = ctx.enter_context(tc.tile_pool(name="opool", bufs=16))
+        opool = ctx.enter_context(tc.tile_pool(name="opool", bufs=22))
         psum = ctx.enter_context(tc.psum_pool(name="psum", bufs=8))
 
         pos_sb = const.tile([P, PASSES, PACK * 2], BF16)
@@ -170,10 +170,12 @@ def tile_gaussiansplatting_t_kernel(tc, positions, activities, position_scale, o
 
         stages = {}
 
-        def product(m, nb):
+        emptied = []
+
+        def product(m, col0, ncols):
             rows = slice(m * P, (m + 1) * P)
-            wcols = slice(nb * 512, (nb + 1) * 512)
-            acc = psum.tile([P, 512], F32, tag="acc")
+            wcols = slice(col0, col0 + ncols)
+            acc = psum.tile([P, ncols], F32, tag="acc")
             for c in range(PASSES):
                 nc.tensor.matmul_mx(
                     out=acc[:],
@@ -181,20 +183,17 @@ def tile_gaussiansplatting_t_kernel(tc, positions, activities, position_scale, o
                     rhs=gx_codes[:, c, wcols].bitcast(FP8X4), rhs_scale=gx_scales[:, c, wcols],
                     start=(c == 0), stop=(c == PASSES - 1),
                 )
-            stage = opool.tile([P, 512], F32, tag="stage")
-            if (2 * m + nb) % 8 != 7:
+            stage = opool.tile([P, ncols], F32, tag="stage")
+            if len(emptied) % 4 != 1:
                 nc.scalar.copy(out=stage[:], in_=acc[:])
             else:
                 nc.vector.tensor_copy(out=stage[:], in_=acc[:])
+            emptied.append(m)
             nc.sync.dma_start(out=out[rows, wcols], in_=stage[:])
 
-        def gx_block(nb):
+        def block(kind, col0, ncols):
             for c in range(PASSES):
-                make(0, c, nb * 512, 512)
-
-        def a_block(col0, ncols):
-            for c in range(PASSES):
-                make(1, c, col0, ncols)
+                make(kind, c, col0, ncols)
 
         make_window(0, 0)
         make(0, 0, 0, 256)
@@ -202,24 +201,26 @@ def tile_gaussiansplatting_t_kernel(tc, positions, activities, position_scale, o
         make(0, 1, 0, 256)
         make_window(1, 0)
         make_window(1, 1)
-        make(0, 0, 256, 256)
-        make(0, 1, 256, 256)
-        a_block(0, 256)
+        block(1, 0, 256)
+        block(0, 256, 256)
         for m in (0, 1):
-            product(m, 0)
-        a_block(256, 256)
+            product(m, 0, 512)
+        block(1, 256, 256)
         for m in (2, 3):
-            product(m, 0)
-        gx_block(1)
+            product(m, 0, 512)
+        block(0, 512, 256)
         for m in (0, 1, 2, 3):
-            product(m, 1)
-        a_block(512, 256)
+            product(m, 512, 256)
+        block(1, 512, 256)
         for m in (4, 5):
-            product(m, 0)
-            product(m, 1)
-        a_block(768, 128)
-        product(6, 0)
-        product(6, 1)
-        a_block(896, 128)
-        product(7, 0)
-        product(7, 1)
+            product(m, 0, 512)
+            product(m, 512, 256)
+        block(0, 768, 256)
+        for m in (0, 1, 2, 3, 4, 5):
+            product(m, 768, 256)
+        block(1, 768, 128)
+        product(6, 0, 512)
+        product(6, 512, 512)
+        block(1, 896, 128)
+        product(7, 0, 512)
+        product(7, 512, 512)

@@ -17,16 +17,18 @@ PACK = 4
 RES = 1024
 NPTS = 1024
 PASSES = NPTS // (P * PACK)
-NCT = PASSES * PACK
-NG = 2 * NCT
-WH = 64
-NCLS = 2
-WF = WH * NCLS
-NM = RES // WF
+GP = 8
+NGRP = RES // GP
+RUN = 4
+NR = NGRP // RUN
 C_PIX = 1250.0 / (1023.0 * 1023.0)
-MAGIC = 1.5 * 2.0 ** 23 * WF
 SHIFT = 0.125
+LIMIT = 8.0
 FLOPS = 2 * RES * RES * NPTS
+
+CH = 256
+CR = CH // (GP * RUN)
+NCH = RES // CH
 
 
 def tile_gaussiansplatting_t_kernel(tc, positions, activities, position_scale, out):
@@ -34,10 +36,11 @@ def tile_gaussiansplatting_t_kernel(tc, positions, activities, position_scale, o
     with ExitStack() as ctx:
         const = ctx.enter_context(tc.tile_pool(name="const", bufs=1))
         keep = ctx.enter_context(tc.tile_pool(name="keep", bufs=1))
-        wpool = ctx.enter_context(tc.tile_pool(name="wpool", bufs=4))
         epool = ctx.enter_context(tc.tile_pool(name="epool", bufs=4))
-        gpool = ctx.enter_context(tc.tile_pool(name="gpool", bufs=3))
-        opool = ctx.enter_context(tc.tile_pool(name="opool", bufs=22))
+        xpool = ctx.enter_context(tc.tile_pool(name="xpool", bufs=3))
+        apool = ctx.enter_context(tc.tile_pool(name="apool", bufs=6))
+        gpool = ctx.enter_context(tc.tile_pool(name="gpool", bufs=4))
+        opool = ctx.enter_context(tc.tile_pool(name="opool", bufs=16))
         psum = ctx.enter_context(tc.psum_pool(name="psum", bufs=8))
 
         pos_sb = const.tile([P, PASSES, PACK * 2], BF16)
@@ -47,180 +50,131 @@ def tile_gaussiansplatting_t_kernel(tc, positions, activities, position_scale, o
         act_sb = const.tile([P, PASSES, PACK], BF16)
         nc.sync.dma_start(out=act_sb[:], in_=activities.rearrange("(c p t) -> p c t", c=PASSES, p=P, t=PACK))
 
-        j_int = const.tile([P, WH], I32)
-        nc.gpsimd.iota(j_int[:], pattern=[[1, WH]], base=0, channel_multiplier=0)
-        j_off = const.tile([P, WH], F32)
-        nc.vector.tensor_scalar(out=j_off[:], in0=j_int[:], scalar1=-(WH - 1) / 2.0, scalar2=None, op0=ALU.add)
-        frame0 = const.tile([P, NM], F32)
-        nc.vector.tensor_scalar(out=frame0[:], in0=j_int[:, 0:NM], scalar1=float(WF), scalar2=None, op0=ALU.mult)
-        sign2 = const.tile([P, 2], F32)
-        nc.vector.memset(sign2[:, 0:1], 1.0)
-        nc.vector.memset(sign2[:, 1:2], -1.0)
-        sign1023 = const.tile([P, 2], F32)
-        nc.vector.memset(sign1023[:, 0:1], 1023.0)
-        nc.vector.memset(sign1023[:, 1:2], -1023.0)
-        rtab = const.tile([P, NCLS], F32)
-        for e in range(NCLS):
-            nc.vector.memset(rtab[:, e:e + 1], 511.5 - (e * WH + (WH - 1) / 2.0))
+        g_int = const.tile([P, NGRP], I32)
+        nc.gpsimd.iota(g_int[:], pattern=[[GP, NGRP]], base=0, channel_multiplier=0)
+        centre = const.tile([P, NR, RUN], F32)
+        nc.vector.tensor_scalar(
+            out=centre[:].rearrange("p r i -> p (r i)"), in0=g_int[:], scalar1=(GP - 1) / 2.0 - 511.5, scalar2=None, op0=ALU.add,
+        )
 
-        pos_v = pos_sb[:].rearrange("p c (t d) -> p (c t) d", d=2)
-        rough = const.tile([P, 2, NCT], F32)
+        raw = const.tile([P, PASSES * PACK, 2], F32)
         nc.vector.scalar_tensor_tensor(
-            out=rough[:].rearrange("p k g -> p g k"), in0=pos_v, scalar=-0.5,
-            in1=sign1023[:].unsqueeze(1).to_broadcast([P, NCT, 2]), op0=ALU.add, op1=ALU.mult,
+            out=raw[:].rearrange("p n d -> p (n d)"), in0=pos_sb[:].rearrange("p c n -> p (c n)"), scalar=-0.5,
+            in1=scl_sb[:].to_broadcast([P, PASSES * PACK * 2]), op0=ALU.add, op1=ALU.mult,
         )
-        rnd = const.tile([P, NCLS, NG], F32)
-        nc.vector.scalar_tensor_tensor(
-            out=rnd[:], in0=rough[:].rearrange("p k g -> p (k g)").unsqueeze(1).to_broadcast([P, NCLS, NG]), scalar=scl_sb[:, 0:1],
-            in1=rtab[:].unsqueeze(2).to_broadcast([P, NCLS, NG]), op0=ALU.mult, op1=ALU.add,
-        )
-        low = const.tile([P, NCLS, NG], F32)
-        nc.vector.tensor_scalar(out=low[:], in0=rnd[:], scalar1=MAGIC, scalar2=MAGIC, op0=ALU.add, op1=ALU.max)
-        s2 = const.tile([P, 2], F32)
-        nc.vector.tensor_scalar(out=s2[:], in0=sign2[:], scalar1=scl_sb[:, 0:1], scalar2=None, op0=ALU.mult)
-        qs = const.tile([P, 2, NCT], F32)
-        nc.vector.scalar_tensor_tensor(
-            out=qs[:].rearrange("p k g -> p g k"), in0=pos_sb[:].rearrange("p c (t d) -> p (c t) d", d=2), scalar=-0.5,
-            in1=s2[:].unsqueeze(1).to_broadcast([P, NCT, 2]), op0=ALU.add, op1=ALU.mult,
-        )
-        qf = qs[:].rearrange("p k g -> p (k g)")
-        q1024 = const.tile([P, NG], F32)
-        nc.vector.tensor_scalar(out=q1024[:], in0=qf, scalar1=-1024.0, scalar2=None, op0=ALU.mult)
-        home = const.tile([P, NCLS, NG], F32)
-        nc.vector.tensor_scalar(out=home[:], in0=low[:], scalar1=MAGIC + float(WF * (NM - 1)), scalar2=-MAGIC, op0=ALU.min, op1=ALU.add)
-        part = const.tile([P, NCLS, NG], F32)
-        nc.vector.tensor_tensor(out=part[:], in0=home[:], in1=q1024[:].unsqueeze(1).to_broadcast([P, NCLS, NG]), op=ALU.add)
-        dref = const.tile([P, NCLS, NG], F32)
-        for e in range(NCLS):
-            first = e * WH + (WH - 1) / 2.0
-            nc.vector.scalar_tensor_tensor(out=dref[:, e, :], in0=part[:, e, :], scalar=first - 511.5, in1=qf, op0=ALU.add, op1=ALU.add)
-        NEG = NCLS * NG
-        hop = const.tile([P, NM, NEG], F32)
-        nc.vector.tensor_tensor(
-            out=hop[:],
-            in0=frame0[:].unsqueeze(2).to_broadcast([P, NM, NEG]),
-            in1=home[:].rearrange("p e g -> p (e g)").unsqueeze(1).to_broadcast([P, NM, NEG]),
-            op=ALU.subtract,
-        )
-        offs = const.tile([P, NM, NEG], F32)
-        nc.vector.scalar_tensor_tensor(out=offs[:], in0=hop[:], scalar=-C_PIX, in1=hop[:], op0=ALU.mult, op1=ALU.mult)
-        slope = const.tile([P, NM, NEG], F32)
-        nc.vector.tensor_scalar(out=slope[:], in0=hop[:], scalar1=-2.0 * C_PIX, scalar2=None, op0=ALU.mult)
+        qs = const.tile([P, PASSES * PACK, 2], F32)
+        nc.vector.tensor_scalar(out=qs[:], in0=raw[:], scalar1=LIMIT, scalar2=-LIMIT, op0=ALU.min, op1=ALU.max)
+        qn = const.tile([P, PASSES * PACK, 2], F32)
+        nc.vector.tensor_scalar(out=qn[:, :, 0:1], in0=qs[:, :, 0:1], scalar1=-1024.0, scalar2=None, op0=ALU.mult)
+        nc.vector.tensor_scalar(out=qn[:, :, 1:2], in0=qs[:, :, 1:2], scalar1=1024.0, scalar2=None, op0=ALU.mult)
 
-        window = const.tile([P, 2, PASSES, WF // 4, PACK, 4], F32)
-        j_runs = j_off[:].rearrange("p (g i) -> p g i", i=4)
-        dists = const.tile([P, 2, PASSES, WF // 4, PACK, 4], F32)
+        dist = const.tile([P, 2, PASSES, NR, PACK, RUN], F32)
+        sq = const.tile([P, 2, PASSES, NR, PACK, RUN], F32)
+        peak = const.tile([P, 2, PASSES, NR, PACK, RUN], F32)
 
-        def make_window(kind, c):
-            dist = dists[:, kind, c]
-            for t in range(PACK):
-                for e in range(NCLS):
-                    gg = kind * NCT + c * PACK + t
+        def distances(kind):
+            for c in range(PASSES):
+                for t in range(PACK):
+                    n = c * PACK + t
                     nc.vector.tensor_scalar(
-                        out=dist[:, e * WH // 4:(e + 1) * WH // 4, t, :], in0=j_runs, scalar1=dref[:, e, gg:gg + 1], scalar2=None, op0=ALU.add,
+                        out=dist[:, kind, c, :, t, :], in0=centre[:], scalar1=qn[:, n, kind:kind + 1], scalar2=qs[:, n, kind:kind + 1],
+                        op0=ALU.add, op1=ALU.add if kind == 0 else ALU.subtract,
                     )
-            sq = wpool.tile([P, WF // 4, PACK, 4], F32, tag="wsq")
-            nc.vector.tensor_tensor(out=sq[:], in0=dist, in1=dist, op=ALU.mult)
-            ea = wpool.tile([P, WF // 4, PACK, 4], F32, tag="wea")
-            nc.scalar.activation(out=ea[:], in_=sq[:], func=ACT.Exp, scale=-C_PIX)
-            eb = wpool.tile([P, WF // 4, PACK, 4], F32, tag="web")
-            nc.scalar.activation(out=eb[:], in_=sq[:], func=ACT.Exp, scale=-C_PIX, bias=SHIFT)
+
+        def square(kind, r0, r1):
+            nc.vector.tensor_tensor(out=sq[:, kind, :, r0:r1], in0=dist[:, kind, :, r0:r1], in1=dist[:, kind, :, r0:r1], op=ALU.mult)
+
+        def peaks(kind, r0, r1):
+            shape = [P, PASSES, r1 - r0, PACK, RUN]
+            ea = epool.tile(shape, F32, tag="ea%d" % (r1 - r0))
+            nc.scalar.activation(out=ea[:], in_=sq[:, kind, :, r0:r1], func=ACT.Exp, scale=-C_PIX)
+            eb = epool.tile(shape, F32, tag="eb%d" % (r1 - r0))
+            nc.scalar.activation(out=eb[:], in_=sq[:, kind, :, r0:r1], func=ACT.Exp, scale=-C_PIX, bias=SHIFT)
             if kind == 0:
-                nc.vector.scalar_tensor_tensor(out=window[:, kind, c], in0=eb[:], scalar=math.exp(-SHIFT), in1=ea[:], op0=ALU.mult, op1=ALU.max)
-            else:
-                best = wpool.tile([P, WF // 4, PACK, 4], F32, tag="wbest")
-                nc.vector.scalar_tensor_tensor(out=best[:], in0=eb[:], scalar=math.exp(-SHIFT), in1=ea[:], op0=ALU.mult, op1=ALU.max)
-                nc.vector.tensor_tensor(
-                    out=window[:, kind, c], in0=best[:],
-                    in1=act_sb[:, c, :].unsqueeze(1).unsqueeze(3).to_broadcast([P, WF // 4, PACK, 4]), op=ALU.mult,
+                nc.vector.scalar_tensor_tensor(
+                    out=peak[:, kind, :, r0:r1], in0=eb[:], scalar=math.exp(-SHIFT), in1=ea[:], op0=ALU.mult, op1=ALU.max,
                 )
+            else:
+                best = epool.tile(shape, F32, tag="best")
+                nc.vector.scalar_tensor_tensor(out=best[:], in0=eb[:], scalar=math.exp(-SHIFT), in1=ea[:], op0=ALU.mult, op1=ALU.max)
+                for c in range(PASSES):
+                    nc.vector.tensor_tensor(
+                        out=peak[:, kind, c, r0:r1], in0=best[:, c],
+                        in1=act_sb[:, c, :].unsqueeze(1).unsqueeze(3).to_broadcast([P, r1 - r0, PACK, RUN]), op=ALU.mult,
+                    )
 
         gx_codes = keep.tile([P, PASSES, RES], U32, align_bytes=64)
         gx_scales = keep.tile([P, PASSES, RES], U8, align_bytes=64)
-        a_codes = keep.tile([P, PASSES, RES], U32, align_bytes=64)
-        a_scales = keep.tile([P, PASSES, RES], U8, align_bytes=64)
+        a_codes = keep.tile([P, GP, PASSES, NGRP], U32, align_bytes=64)
+        a_scales = keep.tile([P, GP, PASSES, NGRP], U8, align_bytes=64)
 
-        def make(kind, c, col0, ncols):
-            codes, scales = (gx_codes, gx_scales) if kind == 0 else (a_codes, a_scales)
-            frames = ncols // WF
-            far = epool.tile([P, ncols // 4, PACK, 4], F32, tag="far%d" % ncols)
-            for t in range(PACK):
-                g = kind * NCT + c * PACK + t
-                for f in range(frames):
-                    m = col0 // WF + f
-                    for e in range(NCLS):
-                        idx = e * NG + g
-                        lo = f * WF + e * WH
-                        nc.scalar.activation(
-                            out=far[:, lo // 4:(lo + WH) // 4, t, :], in_=dists[:, kind, c, e * WH // 4:(e + 1) * WH // 4, t, :], func=ACT.Exp,
-                            bias=offs[:, m, idx:idx + 1], scale=slope[:, m, idx:idx + 1],
-                        )
-            grouped = gpool.tile([P, ncols, PACK], BF16, tag="grouped%d" % ncols, align_bytes=64)
+        def coarse(out_ap, in_ap, v):
+            step = v - (GP - 1) / 2.0
+            nc.scalar.activation(out=out_ap, in_=in_ap, func=ACT.Exp, scale=-2.0 * C_PIX * step, bias=-C_PIX * step * step)
+
+        def make_gx(ch):
+            r0, r1 = ch * CR, (ch + 1) * CR
+            far = xpool.tile([P, PASSES, GP, CR, PACK, RUN], F32, tag="farx")
+            for v in range(GP):
+                coarse(far[:, :, v], dist[:, 0, :, r0:r1], v)
+            for c in range(PASSES):
+                grouped = gpool.tile([P, CH, PACK], BF16, tag="gx", align_bytes=64)
+                nc.vector.tensor_tensor(
+                    out=grouped[:].rearrange("p (v r i) t -> p v r t i", v=GP, i=RUN), in0=far[:, c],
+                    in1=peak[:, 0, c, r0:r1].unsqueeze(1).to_broadcast([P, GP, CR, PACK, RUN]), op=ALU.mult,
+                )
+                cols = slice(ch * CH, (ch + 1) * CH)
+                nc.vector.quantize_mx(
+                    out=gx_codes[:, c, cols].bitcast(FP8X4), scales=gx_scales[:, c, cols], in_=grouped[:].rearrange("p w t -> p (w t)"),
+                )
+
+        def make_a(v):
+            far = apool.tile([P, PASSES, NR, PACK, RUN], F32, tag="fara")
+            coarse(far[:], dist[:, 1], v)
+            grouped = gpool.tile([P, PASSES * NGRP, PACK], BF16, tag="a", align_bytes=64)
             nc.vector.tensor_tensor(
-                out=grouped[:].rearrange("p (f g i) t -> p f g t i", f=frames, i=4),
-                in0=far[:].rearrange("p (f g) t i -> p f g t i", f=frames),
-                in1=window[:, kind, c].unsqueeze(1).to_broadcast([P, frames, WF // 4, PACK, 4]),
-                op=ALU.mult,
+                out=grouped[:].rearrange("p (c r i) t -> p (c r) t i", c=PASSES, i=RUN), in0=far[:].rearrange("p c r t i -> p (c r) t i"),
+                in1=peak[:, 1].rearrange("p c r t i -> p (c r) t i"), op=ALU.mult,
             )
-            cols = slice(col0, col0 + ncols)
             nc.vector.quantize_mx(
-                out=codes[:, c, cols].bitcast(FP8X4), scales=scales[:, c, cols],
+                out=a_codes[:, v].rearrange("p c g -> p (c g)").bitcast(FP8X4), scales=a_scales[:, v].rearrange("p c g -> p (c g)"),
                 in_=grouped[:].rearrange("p w t -> p (w t)"),
             )
 
-        stages = {}
+        out_rows = out.rearrange("(g v) w -> v g w", v=GP)
 
-        emptied = []
-
-        def product(m, col0, ncols):
-            rows = slice(m * P, (m + 1) * P)
-            wcols = slice(col0, col0 + ncols)
-            acc = psum.tile([P, ncols], F32, tag="acc")
+        def product(v, half):
+            acc = psum.tile([P, RES // 2], F32, tag="acc")
+            wcols = slice(half * RES // 2, (half + 1) * RES // 2)
             for c in range(PASSES):
                 nc.tensor.matmul_mx(
                     out=acc[:],
-                    lhsT=a_codes[:, c, rows].bitcast(FP8X4), lhsT_scale=a_scales[:, c, rows],
+                    lhsT=a_codes[:, v, c].bitcast(FP8X4), lhsT_scale=a_scales[:, v, c],
                     rhs=gx_codes[:, c, wcols].bitcast(FP8X4), rhs_scale=gx_scales[:, c, wcols],
                     start=(c == 0), stop=(c == PASSES - 1),
                 )
-            stage = opool.tile([P, ncols], F32, tag="stage")
-            if len(emptied) % 4 != 1:
-                nc.scalar.copy(out=stage[:], in_=acc[:])
+            stage = opool.tile([P, RES // 2], F32, tag="stage")
+            src = acc[:].rearrange("p (h v g) -> p h g v", v=GP, g=CR * RUN)
+            dst = stage[:].rearrange("p (h g v) -> p h g v", v=GP, g=CR * RUN)
+            if (2 * v + half) % 8 == 7:
+                nc.vector.tensor_copy(out=dst, in_=src)
             else:
-                nc.vector.tensor_copy(out=stage[:], in_=acc[:])
-            emptied.append(m)
-            nc.sync.dma_start(out=out[rows, wcols], in_=stage[:])
+                nc.scalar.copy(out=dst, in_=src)
+            nc.sync.dma_start(out=out_rows[v][:, wcols], in_=stage[:])
 
-        def block(kind, col0, ncols):
-            for c in range(PASSES):
-                make(kind, c, col0, ncols)
-
-        make_window(0, 0)
-        make(0, 0, 0, 256)
-        make_window(0, 1)
-        make(0, 1, 0, 256)
-        make_window(1, 0)
-        make_window(1, 1)
-        block(1, 0, 256)
-        block(0, 256, 256)
-        for m in (0, 1):
-            product(m, 0, 512)
-        block(1, 256, 256)
-        for m in (2, 3):
-            product(m, 0, 512)
-        block(0, 512, 256)
-        for m in (0, 1, 2, 3):
-            product(m, 512, 256)
-        block(1, 512, 256)
-        for m in (4, 5):
-            product(m, 0, 512)
-            product(m, 512, 256)
-        block(0, 768, 256)
-        for m in (0, 1, 2, 3, 4, 5):
-            product(m, 768, 256)
-        block(1, 768, 128)
-        product(6, 0, 512)
-        product(6, 512, 512)
-        block(1, 896, 128)
-        product(7, 0, 512)
-        product(7, 512, 512)
+        distances(0)
+        square(0, 0, CR)
+        peaks(0, 0, CR)
+        square(0, CR, NR)
+        make_gx(0)
+        distances(1)
+        peaks(0, CR, NR)
+        make_gx(1)
+        square(1, 0, NR)
+        make_gx(2)
+        peaks(1, 0, NR)
+        make_gx(3)
+        for v in range(GP):
+            make_a(v)
+            for half in range(2):
+                product(v, half)

@@ -26,9 +26,7 @@ SHIFT = 0.125
 LIMIT = 8.0
 FLOPS = 2 * RES * RES * NPTS
 
-CH = 256
-CR = CH // (GP * RUN)
-NCH = RES // CH
+HV = GP // 2
 
 
 def tile_gaussiansplatting_t_kernel(tc, positions, activities, position_scale, out):
@@ -37,10 +35,10 @@ def tile_gaussiansplatting_t_kernel(tc, positions, activities, position_scale, o
         const = ctx.enter_context(tc.tile_pool(name="const", bufs=1))
         keep = ctx.enter_context(tc.tile_pool(name="keep", bufs=1))
         epool = ctx.enter_context(tc.tile_pool(name="epool", bufs=4))
-        xpool = ctx.enter_context(tc.tile_pool(name="xpool", bufs=3))
+        xpool = ctx.enter_context(tc.tile_pool(name="xpool", bufs=8))
         apool = ctx.enter_context(tc.tile_pool(name="apool", bufs=6))
         gpool = ctx.enter_context(tc.tile_pool(name="gpool", bufs=4))
-        opool = ctx.enter_context(tc.tile_pool(name="opool", bufs=16))
+        opool = ctx.enter_context(tc.tile_pool(name="opool", bufs=8))
         psum = ctx.enter_context(tc.psum_pool(name="psum", bufs=8))
 
         pos_sb = const.tile([P, PASSES, PACK * 2], BF16)
@@ -72,36 +70,30 @@ def tile_gaussiansplatting_t_kernel(tc, positions, activities, position_scale, o
         sq = const.tile([P, 2, PASSES, NR, PACK, RUN], F32)
         peak = const.tile([P, 2, PASSES, NR, PACK, RUN], F32)
 
-        def distances(kind):
-            for c in range(PASSES):
-                for t in range(PACK):
-                    n = c * PACK + t
-                    nc.vector.tensor_scalar(
-                        out=dist[:, kind, c, :, t, :], in0=centre[:], scalar1=qn[:, n, kind:kind + 1], scalar2=qs[:, n, kind:kind + 1],
-                        op0=ALU.add, op1=ALU.add if kind == 0 else ALU.subtract,
-                    )
-
-        def square(kind, r0, r1):
-            nc.vector.tensor_tensor(out=sq[:, kind, :, r0:r1], in0=dist[:, kind, :, r0:r1], in1=dist[:, kind, :, r0:r1], op=ALU.mult)
-
-        def peaks(kind, r0, r1):
-            shape = [P, PASSES, r1 - r0, PACK, RUN]
-            ea = epool.tile(shape, F32, tag="ea%d" % (r1 - r0))
-            nc.scalar.activation(out=ea[:], in_=sq[:, kind, :, r0:r1], func=ACT.Exp, scale=-C_PIX)
-            eb = epool.tile(shape, F32, tag="eb%d" % (r1 - r0))
-            nc.scalar.activation(out=eb[:], in_=sq[:, kind, :, r0:r1], func=ACT.Exp, scale=-C_PIX, bias=SHIFT)
-            if kind == 0:
-                nc.vector.scalar_tensor_tensor(
-                    out=peak[:, kind, :, r0:r1], in0=eb[:], scalar=math.exp(-SHIFT), in1=ea[:], op0=ALU.mult, op1=ALU.max,
+        def distances(kind, c):
+            for t in range(PACK):
+                n = c * PACK + t
+                nc.vector.tensor_scalar(
+                    out=dist[:, kind, c, :, t, :], in0=centre[:], scalar1=qn[:, n, kind:kind + 1], scalar2=qs[:, n, kind:kind + 1],
+                    op0=ALU.add, op1=ALU.add if kind == 0 else ALU.subtract,
                 )
-            else:
-                best = epool.tile(shape, F32, tag="best")
-                nc.vector.scalar_tensor_tensor(out=best[:], in0=eb[:], scalar=math.exp(-SHIFT), in1=ea[:], op0=ALU.mult, op1=ALU.max)
-                for c in range(PASSES):
-                    nc.vector.tensor_tensor(
-                        out=peak[:, kind, c, r0:r1], in0=best[:, c],
-                        in1=act_sb[:, c, :].unsqueeze(1).unsqueeze(3).to_broadcast([P, r1 - r0, PACK, RUN]), op=ALU.mult,
-                    )
+
+        def peaks(kind, c):
+            nc.vector.tensor_tensor(out=sq[:, kind, c], in0=dist[:, kind, c], in1=dist[:, kind, c], op=ALU.mult)
+            ea = epool.tile([P, NR, PACK, RUN], F32, tag="ea")
+            nc.scalar.activation(out=ea[:], in_=sq[:, kind, c], func=ACT.Exp, scale=-C_PIX)
+            eb = epool.tile([P, NR, PACK, RUN], F32, tag="eb")
+            nc.scalar.activation(out=eb[:], in_=sq[:, kind, c], func=ACT.Exp, scale=-C_PIX, bias=SHIFT)
+            best = peak[:, kind, c]
+            if kind == 1:
+                best_tile = epool.tile([P, NR, PACK, RUN], F32, tag="best")
+                best = best_tile[:]
+            nc.vector.scalar_tensor_tensor(out=best, in0=eb[:], scalar=math.exp(-SHIFT), in1=ea[:], op0=ALU.mult, op1=ALU.max)
+            if kind == 1:
+                nc.vector.tensor_tensor(
+                    out=peak[:, kind, c], in0=best,
+                    in1=act_sb[:, c, :].unsqueeze(1).unsqueeze(3).to_broadcast([P, NR, PACK, RUN]), op=ALU.mult,
+                )
 
         gx_codes = keep.tile([P, PASSES, RES], U32, align_bytes=64)
         gx_scales = keep.tile([P, PASSES, RES], U8, align_bytes=64)
@@ -112,21 +104,19 @@ def tile_gaussiansplatting_t_kernel(tc, positions, activities, position_scale, o
             step = v - (GP - 1) / 2.0
             nc.scalar.activation(out=out_ap, in_=in_ap, func=ACT.Exp, scale=-2.0 * C_PIX * step, bias=-C_PIX * step * step)
 
-        def make_gx(ch):
-            r0, r1 = ch * CR, (ch + 1) * CR
-            far = xpool.tile([P, PASSES, GP, CR, PACK, RUN], F32, tag="farx")
-            for v in range(GP):
-                coarse(far[:, :, v], dist[:, 0, :, r0:r1], v)
-            for c in range(PASSES):
-                grouped = gpool.tile([P, CH, PACK], BF16, tag="gx", align_bytes=64)
+        def make_gx(c, v0):
+            grouped = gpool.tile([P, 2 * NGRP, PACK], BF16, tag="gx", align_bytes=64)
+            for v in (v0, v0 + 1):
+                far = xpool.tile([P, NR, PACK, RUN], F32, tag="farx")
+                coarse(far[:], dist[:, 0, c], v)
                 nc.vector.tensor_tensor(
-                    out=grouped[:].rearrange("p (v r i) t -> p v r t i", v=GP, i=RUN), in0=far[:, c],
-                    in1=peak[:, 0, c, r0:r1].unsqueeze(1).to_broadcast([P, GP, CR, PACK, RUN]), op=ALU.mult,
+                    out=grouped[:, (v - v0) * NGRP:(v - v0 + 1) * NGRP, :].rearrange("p (r i) t -> p r t i", i=RUN),
+                    in0=far[:], in1=peak[:, 0, c], op=ALU.mult,
                 )
-                cols = slice(ch * CH, (ch + 1) * CH)
-                nc.vector.quantize_mx(
-                    out=gx_codes[:, c, cols].bitcast(FP8X4), scales=gx_scales[:, c, cols], in_=grouped[:].rearrange("p w t -> p (w t)"),
-                )
+            cols = slice(v0 * NGRP, (v0 + 2) * NGRP)
+            nc.vector.quantize_mx(
+                out=gx_codes[:, c, cols].bitcast(FP8X4), scales=gx_scales[:, c, cols], in_=grouped[:].rearrange("p w t -> p (w t)"),
+            )
 
         def make_a(v):
             far = apool.tile([P, PASSES, NR, PACK, RUN], F32, tag="fara")
@@ -143,38 +133,42 @@ def tile_gaussiansplatting_t_kernel(tc, positions, activities, position_scale, o
 
         out_rows = out.rearrange("(g v) w -> v g w", v=GP)
 
-        def product(v, half):
-            acc = psum.tile([P, RES // 2], F32, tag="acc")
-            wcols = slice(half * RES // 2, (half + 1) * RES // 2)
-            for c in range(PASSES):
-                nc.tensor.matmul_mx(
-                    out=acc[:],
-                    lhsT=a_codes[:, v, c].bitcast(FP8X4), lhsT_scale=a_scales[:, v, c],
-                    rhs=gx_codes[:, c, wcols].bitcast(FP8X4), rhs_scale=gx_scales[:, c, wcols],
-                    start=(c == 0), stop=(c == PASSES - 1),
-                )
-            stage = opool.tile([P, RES // 2], F32, tag="stage")
-            src = acc[:].rearrange("p (h v g) -> p h g v", v=GP, g=CR * RUN)
-            dst = stage[:].rearrange("p (h g v) -> p h g v", v=GP, g=CR * RUN)
-            if (2 * v + half) % 8 == 7:
-                nc.vector.tensor_copy(out=dst, in_=src)
-            else:
-                nc.scalar.copy(out=dst, in_=src)
-            nc.sync.dma_start(out=out_rows[v][:, wcols], in_=stage[:])
+        def product(v):
+            stage = opool.tile([P, NR, RUN, GP], F32, tag="stage")
+            for half in range(2):
+                acc = psum.tile([P, HV, NR, RUN], F32, tag="acc")
+                cols = slice(half * HV * NGRP, (half + 1) * HV * NGRP)
+                for c in range(PASSES):
+                    nc.tensor.matmul_mx(
+                        out=acc[:].rearrange("p v r i -> p (v r i)"),
+                        lhsT=a_codes[:, v, c].bitcast(FP8X4), lhsT_scale=a_scales[:, v, c],
+                        rhs=gx_codes[:, c, cols].bitcast(FP8X4), rhs_scale=gx_scales[:, c, cols],
+                        start=(c == 0), stop=(c == PASSES - 1),
+                    )
+                src = acc[:].rearrange("p v r i -> p r v i")
+                dst = stage[:, :, :, half * HV:(half + 1) * HV].rearrange("p r i v -> p r v i")
+                if (2 * v + half) % 8 == 7:
+                    nc.vector.tensor_copy(out=dst, in_=src)
+                else:
+                    nc.scalar.copy(out=dst, in_=src)
+            nc.sync.dma_start(out=out_rows[v], in_=stage[:].rearrange("p r i v -> p (r i v)"))
 
-        distances(0)
-        square(0, 0, CR)
-        peaks(0, 0, CR)
-        square(0, CR, NR)
-        make_gx(0)
-        distances(1)
-        peaks(0, CR, NR)
-        make_gx(1)
-        square(1, 0, NR)
-        make_gx(2)
-        peaks(1, 0, NR)
-        make_gx(3)
+        distances(0, 0)
+        peaks(0, 0)
+        make_gx(0, 0)
+        distances(0, 1)
+        make_gx(0, 2)
+        peaks(0, 1)
+        make_gx(0, 4)
+        distances(1, 0)
+        distances(1, 1)
+        make_gx(0, 6)
+        make_gx(1, 0)
+        make_gx(1, 2)
+        peaks(1, 0)
+        make_gx(1, 4)
+        peaks(1, 1)
+        make_gx(1, 6)
         for v in range(GP):
             make_a(v)
-            for half in range(2):
-                product(v, half)
+            product(v)

@@ -26,7 +26,10 @@ SHIFT = 0.125
 LIMIT = 8.0
 FLOPS = 2 * RES * RES * NPTS
 
-HV = GP // 2
+HALF = RES // 2
+HR = NR // 2
+HG = NGRP // 2
+QUAD = GP // 2
 
 
 def tile_gaussiansplatting_t_kernel(tc, positions, activities, position_scale, out):
@@ -35,11 +38,12 @@ def tile_gaussiansplatting_t_kernel(tc, positions, activities, position_scale, o
         const = ctx.enter_context(tc.tile_pool(name="const", bufs=1))
         keep = ctx.enter_context(tc.tile_pool(name="keep", bufs=1))
         epool = ctx.enter_context(tc.tile_pool(name="epool", bufs=4))
-        xpool = ctx.enter_context(tc.tile_pool(name="xpool", bufs=8))
-        apool = ctx.enter_context(tc.tile_pool(name="apool", bufs=6))
+        xpool = ctx.enter_context(tc.tile_pool(name="xpool", bufs=2))
+        apool = ctx.enter_context(tc.tile_pool(name="apool", bufs=8))
         gpool = ctx.enter_context(tc.tile_pool(name="gpool", bufs=4))
-        opool = ctx.enter_context(tc.tile_pool(name="opool", bufs=8))
+        opool = ctx.enter_context(tc.tile_pool(name="opool", bufs=16))
         psum = ctx.enter_context(tc.psum_pool(name="psum", bufs=8))
+        ctx.enter_context(tc.manual_schedule())
 
         pos_sb = const.tile([P, PASSES, PACK * 2], BF16)
         nc.sync.dma_start(out=pos_sb[:], in_=positions.rearrange("(c p t) d -> p c (t d)", c=PASSES, p=P, t=PACK))
@@ -78,22 +82,18 @@ def tile_gaussiansplatting_t_kernel(tc, positions, activities, position_scale, o
                     op0=ALU.add, op1=ALU.add if kind == 0 else ALU.subtract,
                 )
 
-        def peaks(kind, c):
+        def squares(kind, c):
             nc.vector.tensor_tensor(out=sq[:, kind, c], in0=dist[:, kind, c], in1=dist[:, kind, c], op=ALU.mult)
+
+        def peak_exps(kind, c):
             ea = epool.tile([P, NR, PACK, RUN], F32, tag="ea")
             nc.scalar.activation(out=ea[:], in_=sq[:, kind, c], func=ACT.Exp, scale=-C_PIX)
             eb = epool.tile([P, NR, PACK, RUN], F32, tag="eb")
             nc.scalar.activation(out=eb[:], in_=sq[:, kind, c], func=ACT.Exp, scale=-C_PIX, bias=SHIFT)
-            best = peak[:, kind, c]
-            if kind == 1:
-                best_tile = epool.tile([P, NR, PACK, RUN], F32, tag="best")
-                best = best_tile[:]
-            nc.vector.scalar_tensor_tensor(out=best, in0=eb[:], scalar=math.exp(-SHIFT), in1=ea[:], op0=ALU.mult, op1=ALU.max)
-            if kind == 1:
-                nc.vector.tensor_tensor(
-                    out=peak[:, kind, c], in0=best,
-                    in1=act_sb[:, c, :].unsqueeze(1).unsqueeze(3).to_broadcast([P, NR, PACK, RUN]), op=ALU.mult,
-                )
+            return ea, eb
+
+        def larger(out_ap, pair):
+            nc.vector.scalar_tensor_tensor(out=out_ap, in0=pair[1][:], scalar=math.exp(-SHIFT), in1=pair[0][:], op0=ALU.mult, op1=ALU.max)
 
         gx_codes = keep.tile([P, PASSES, RES], U32, align_bytes=64)
         gx_scales = keep.tile([P, PASSES, RES], U8, align_bytes=64)
@@ -104,71 +104,148 @@ def tile_gaussiansplatting_t_kernel(tc, positions, activities, position_scale, o
             step = v - (GP - 1) / 2.0
             nc.scalar.activation(out=out_ap, in_=in_ap, func=ACT.Exp, scale=-2.0 * C_PIX * step, bias=-C_PIX * step * step)
 
-        def make_gx(c, v0):
-            grouped = gpool.tile([P, 2 * NGRP, PACK], BF16, tag="gx", align_bytes=64)
-            for v in (v0, v0 + 1):
-                far = xpool.tile([P, NR, PACK, RUN], F32, tag="farx")
-                coarse(far[:], dist[:, 0, c], v)
-                nc.vector.tensor_tensor(
-                    out=grouped[:, (v - v0) * NGRP:(v - v0 + 1) * NGRP, :].rearrange("p (r i) t -> p r t i", i=RUN),
-                    in0=far[:], in1=peak[:, 0, c], op=ALU.mult,
-                )
-            cols = slice(v0 * NGRP, (v0 + 2) * NGRP)
-            nc.vector.quantize_mx(
-                out=gx_codes[:, c, cols].bitcast(FP8X4), scales=gx_scales[:, c, cols], in_=grouped[:].rearrange("p w t -> p (w t)"),
-            )
+        def coarse_gx(far, h, v0, v1):
+            for v in range(v0, v1):
+                coarse(far[:, :, v], dist[:, 0, :, h * HR:(h + 1) * HR], v)
 
-        def make_a(v):
+        def coarse_a(v):
             far = apool.tile([P, PASSES, NR, PACK, RUN], F32, tag="fara")
             coarse(far[:], dist[:, 1], v)
-            grouped = gpool.tile([P, PASSES * NGRP, PACK], BF16, tag="a", align_bytes=64)
+            return far
+
+        def quad_gx(h, far, u):
+            tiles = []
+            for c in range(PASSES):
+                g_tile = gpool.tile([P, QUAD * HG, PACK], BF16, tag="gx", align_bytes=64)
+                tiles.append(g_tile)
+            for j in range(0, QUAD, 2):
+                for c in range(PASSES):
+                    v = u * QUAD + j
+                    nc.vector.tensor_tensor(
+                        out=tiles[c][:, j * HG:(j + 2) * HG, :].rearrange("p (v r i) t -> p v r t i", v=2, i=RUN), in0=far[:, c, v:v + 2],
+                        in1=peak[:, 0, c, h * HR:(h + 1) * HR].unsqueeze(1).to_broadcast([P, 2, HR, PACK, RUN]), op=ALU.mult,
+                    )
+            for c in range(PASSES):
+                cols = slice(h * HALF + u * QUAD * HG, h * HALF + (u + 1) * QUAD * HG)
+                nc.vector.quantize_mx(
+                    out=gx_codes[:, c, cols].bitcast(FP8X4), scales=gx_scales[:, c, cols], in_=tiles[c][:].rearrange("p w t -> p (w t)"),
+                )
+
+        a_grouped = {}
+
+        def mult_a(v, c, far):
+            grouped = gpool.tile([P, NGRP, PACK], BF16, tag="a", align_bytes=64)
             nc.vector.tensor_tensor(
-                out=grouped[:].rearrange("p (c r i) t -> p (c r) t i", c=PASSES, i=RUN), in0=far[:].rearrange("p c r t i -> p (c r) t i"),
-                in1=peak[:, 1].rearrange("p c r t i -> p (c r) t i"), op=ALU.mult,
+                out=grouped[:].rearrange("p (r i) t -> p r t i", i=RUN), in0=far[:, c], in1=peak[:, 1, c], op=ALU.mult,
             )
+            a_grouped[v, c] = grouped
+
+        def quant_a(v, c):
             nc.vector.quantize_mx(
-                out=a_codes[:, v].rearrange("p c g -> p (c g)").bitcast(FP8X4), scales=a_scales[:, v].rearrange("p c g -> p (c g)"),
-                in_=grouped[:].rearrange("p w t -> p (w t)"),
+                out=a_codes[:, v, c].bitcast(FP8X4), scales=a_scales[:, v, c], in_=a_grouped[v, c][:].rearrange("p w t -> p (w t)"),
+            )
+
+        accs = {}
+
+        def open_bank(v, h):
+            acc = psum.tile([P, GP, HR, RUN], F32, tag="acc")
+            accs[v, h] = acc
+
+        def one_pass(v, h, c, v0=0, v1=GP):
+            cols = slice(h * HALF + v0 * HG, h * HALF + v1 * HG)
+            nc.tensor.matmul_mx(
+                out=accs[v, h][:, v0:v1].rearrange("p v r i -> p (v r i)"),
+                lhsT=a_codes[:, v, c].bitcast(FP8X4), lhsT_scale=a_scales[:, v, c],
+                rhs=gx_codes[:, c, cols].bitcast(FP8X4), rhs_scale=gx_scales[:, c, cols],
+                start=(c == 0), stop=(c == PASSES - 1),
             )
 
         out_rows = out.rearrange("(g v) w -> v g w", v=GP)
 
-        def product(v):
-            stage = opool.tile([P, NR, RUN, GP], F32, tag="stage")
-            for half in range(2):
-                acc = psum.tile([P, HV, NR, RUN], F32, tag="acc")
-                cols = slice(half * HV * NGRP, (half + 1) * HV * NGRP)
-                for c in range(PASSES):
-                    nc.tensor.matmul_mx(
-                        out=acc[:].rearrange("p v r i -> p (v r i)"),
-                        lhsT=a_codes[:, v, c].bitcast(FP8X4), lhsT_scale=a_scales[:, v, c],
-                        rhs=gx_codes[:, c, cols].bitcast(FP8X4), rhs_scale=gx_scales[:, c, cols],
-                        start=(c == 0), stop=(c == PASSES - 1),
-                    )
-                src = acc[:].rearrange("p v r i -> p r v i")
-                dst = stage[:, :, :, half * HV:(half + 1) * HV].rearrange("p r i v -> p r v i")
-                if (2 * v + half) % 8 == 7:
-                    nc.vector.tensor_copy(out=dst, in_=src)
-                else:
-                    nc.scalar.copy(out=dst, in_=src)
-            nc.sync.dma_start(out=out_rows[v], in_=stage[:].rearrange("p r i v -> p (r i v)"))
+        def empty(v, h, copy):
+            stage = opool.tile([P, HR, RUN, GP], F32, tag="stage")
+            copy(out=stage[:].rearrange("p r i v -> p r v i"), in_=accs[v, h][:].rearrange("p v r i -> p r v i"))
+            nc.sync.dma_start(out=out_rows[v][:, h * HALF:(h + 1) * HALF], in_=stage[:].rearrange("p r i v -> p (r i v)"))
 
         distances(0, 0)
-        peaks(0, 0)
-        make_gx(0, 0)
         distances(0, 1)
-        make_gx(0, 2)
-        peaks(0, 1)
-        make_gx(0, 4)
+        squares(0, 0)
+        squares(0, 1)
+        far_x0 = xpool.tile([P, PASSES, GP, HR, PACK, RUN], F32, tag="farx")
+        coarse_gx(far_x0, 0, 0, 1)
+        x0 = peak_exps(0, 0)
+        x1 = peak_exps(0, 1)
+        coarse_gx(far_x0, 0, 1, GP)
         distances(1, 0)
         distances(1, 1)
-        make_gx(0, 6)
-        make_gx(1, 0)
-        make_gx(1, 2)
-        peaks(1, 0)
-        make_gx(1, 4)
-        peaks(1, 1)
-        make_gx(1, 6)
-        for v in range(GP):
-            make_a(v)
-            product(v)
+        larger(peak[:, 0, 0], x0)
+        squares(1, 0)
+        larger(peak[:, 0, 1], x1)
+        squares(1, 1)
+        y_pairs = [peak_exps(1, c) for c in range(PASSES)]
+        far_a = [coarse_a(v) for v in range(GP // 2)]
+        far_x1 = xpool.tile([P, PASSES, GP, HR, PACK, RUN], F32, tag="farx")
+        coarse_gx(far_x1, 1, 0, GP)
+
+        quad_gx(0, far_x0, 0)
+        best = []
+        for c in range(PASSES):
+            b_tile = epool.tile([P, NR, PACK, RUN], F32, tag="best")
+            best.append(b_tile)
+        quad_gx(0, far_x0, 1)
+        for c in range(PASSES):
+            larger(best[c][:], y_pairs[c])
+        for c in range(PASSES):
+            nc.vector.tensor_tensor(
+                out=peak[:, 1, c], in0=best[c][:],
+                in1=act_sb[:, c, :].unsqueeze(1).unsqueeze(3).to_broadcast([P, NR, PACK, RUN]), op=ALU.mult,
+            )
+
+        for v in range(GP // 2):
+            open_bank(v, 0)
+            mult_a(v, 0, far_a[v])
+            if v > 0:
+                quant_a(v - 1, 1)
+                one_pass(v - 1, 0, 1)
+            mult_a(v, 1, far_a[v])
+            quant_a(v, 0)
+            one_pass(v, 0, 0)
+        quant_a(GP // 2 - 1, 1)
+        one_pass(GP // 2 - 1, 0, 1)
+
+        for v in range(GP // 2):
+            open_bank(v, 1)
+        for u in range(GP // QUAD):
+            quad_gx(1, far_x1, u)
+            for v in range(GP // 2):
+                for c in range(PASSES):
+                    one_pass(v, 1, c, u * QUAD, (u + 1) * QUAD)
+        for v in range(GP // 2):
+            empty(v, 0, nc.scalar.copy)
+        far_a += [coarse_a(v) for v in range(GP // 2, GP)]
+        for v in range(GP // 2):
+            empty(v, 1, nc.scalar.copy)
+
+        for v in range(GP // 2, GP):
+            for h in range(2):
+                open_bank(v, h)
+            mult_a(v, 0, far_a[v])
+            if v > GP // 2:
+                quant_a(v - 1, 1)
+                for h in range(2):
+                    one_pass(v - 1, h, 1)
+                    empty(v - 1, h, nc.scalar.copy)
+            if v < GP - 1:
+                mult_a(v, 1, far_a[v])
+                quant_a(v, 0)
+            else:
+                quant_a(v, 0)
+                mult_a(v, 1, far_a[v])
+            for h in range(2):
+                one_pass(v, h, 0)
+        v = GP - 1
+        quant_a(v, 1)
+        for h in range(2):
+            one_pass(v, h, 1)
+        empty(v, 0, nc.scalar.copy)
+        empty(v, 1, nc.vector.tensor_copy)

@@ -18,9 +18,11 @@ RES = 1024
 NPTS = 1024
 PASSES = NPTS // (P * PACK)
 GP = 8
+GA = 16
 NGRP = RES // GP
 RUN = 4
 NR = NGRP // RUN
+NRUNS = (NR, RES // (GA * RUN))
 C_PIX = 1250.0 / (1023.0 * 1023.0)
 SHIFT = 0.125
 LIMIT = 8.0
@@ -53,11 +55,15 @@ def tile_gaussiansplatting_t_kernel(tc, positions, activities, position_scale, o
         nc.sync.dma_start(out=act_sb[:], in_=activities.rearrange("(c p t) -> p c t", c=PASSES, p=P, t=PACK))
 
         g_int = const.tile([P, NGRP], I32)
-        nc.gpsimd.iota(g_int[:], pattern=[[GP, NGRP]], base=0, channel_multiplier=0)
-        centre = const.tile([P, NR, RUN], F32)
-        nc.vector.tensor_scalar(
-            out=centre[:].rearrange("p r i -> p (r i)"), in0=g_int[:], scalar1=(GP - 1) / 2.0 - 511.5, scalar2=None, op0=ALU.add,
-        )
+        nc.gpsimd.iota(g_int[:], pattern=[[1, NGRP]], base=0, channel_multiplier=0)
+        centre = []
+        for size in (GP, GA):
+            tab = const.tile([P, RES // (size * RUN), RUN], F32, name="centre%d" % size)
+            nc.vector.tensor_scalar(
+                out=tab[:].rearrange("p r i -> p (r i)"), in0=g_int[:, 0:RES // size],
+                scalar1=float(size), scalar2=(size - 1) / 2.0 - 511.5, op0=ALU.mult, op1=ALU.add,
+            )
+            centre.append(tab)
 
         raw = const.tile([P, PASSES * PACK, 2], F32)
         nc.vector.scalar_tensor_tensor(
@@ -70,26 +76,32 @@ def tile_gaussiansplatting_t_kernel(tc, positions, activities, position_scale, o
         nc.vector.tensor_scalar(out=qn[:, :, 0:1], in0=qs[:, :, 0:1], scalar1=-1024.0, scalar2=None, op0=ALU.mult)
         nc.vector.tensor_scalar(out=qn[:, :, 1:2], in0=qs[:, :, 1:2], scalar1=1024.0, scalar2=None, op0=ALU.mult)
 
-        dist = const.tile([P, 2, PASSES, NR, PACK, RUN], F32)
-        sq = const.tile([P, 2, PASSES, NR, PACK, RUN], F32)
-        peak = const.tile([P, 2, PASSES, NR, PACK, RUN], F32)
+        dist, sq, peak = [], [], []
+        for kind in range(2):
+            shape = [P, PASSES, NRUNS[kind], PACK, RUN]
+            d_tile = const.tile(shape, F32, name="dist%d" % kind)
+            dist.append(d_tile)
+            s_tile = const.tile(shape, F32, name="sq%d" % kind)
+            sq.append(s_tile)
+            p_tile = const.tile(shape, F32, name="peak%d" % kind)
+            peak.append(p_tile)
 
         def distances(kind, c):
             for t in range(PACK):
                 n = c * PACK + t
                 nc.vector.tensor_scalar(
-                    out=dist[:, kind, c, :, t, :], in0=centre[:], scalar1=qn[:, n, kind:kind + 1], scalar2=qs[:, n, kind:kind + 1],
+                    out=dist[kind][:, c, :, t, :], in0=centre[kind][:], scalar1=qn[:, n, kind:kind + 1], scalar2=qs[:, n, kind:kind + 1],
                     op0=ALU.add, op1=ALU.add if kind == 0 else ALU.subtract,
                 )
 
         def squares(kind, c):
-            nc.vector.tensor_tensor(out=sq[:, kind, c], in0=dist[:, kind, c], in1=dist[:, kind, c], op=ALU.mult)
+            nc.vector.tensor_tensor(out=sq[kind][:, c], in0=dist[kind][:, c], in1=dist[kind][:, c], op=ALU.mult)
 
         def peak_exps(kind, c):
-            ea = epool.tile([P, NR, PACK, RUN], F32, tag="ea")
-            nc.scalar.activation(out=ea[:], in_=sq[:, kind, c], func=ACT.Exp, scale=-C_PIX)
-            eb = epool.tile([P, NR, PACK, RUN], F32, tag="eb")
-            nc.scalar.activation(out=eb[:], in_=sq[:, kind, c], func=ACT.Exp, scale=-C_PIX, bias=SHIFT)
+            ea = epool.tile([P, NRUNS[kind], PACK, RUN], F32, tag="ea%d" % kind)
+            nc.scalar.activation(out=ea[:], in_=sq[kind][:, c], func=ACT.Exp, scale=-C_PIX)
+            eb = epool.tile([P, NRUNS[kind], PACK, RUN], F32, tag="eb%d" % kind)
+            nc.scalar.activation(out=eb[:], in_=sq[kind][:, c], func=ACT.Exp, scale=-C_PIX, bias=SHIFT)
             return ea, eb
 
         def larger(out_ap, pair):
@@ -100,17 +112,17 @@ def tile_gaussiansplatting_t_kernel(tc, positions, activities, position_scale, o
         a_codes = keep.tile([P, GP, PASSES, NGRP], U32, align_bytes=64)
         a_scales = keep.tile([P, GP, PASSES, NGRP], U8, align_bytes=64)
 
-        def coarse(out_ap, in_ap, v):
-            step = v - (GP - 1) / 2.0
+        def coarse(out_ap, in_ap, step):
             nc.scalar.activation(out=out_ap, in_=in_ap, func=ACT.Exp, scale=-2.0 * C_PIX * step, bias=-C_PIX * step * step)
 
         def coarse_gx(far, h, v0, v1):
             for v in range(v0, v1):
-                coarse(far[:, :, v], dist[:, 0, :, h * HR:(h + 1) * HR], v)
+                coarse(far[:, :, v], dist[0][:, :, h * HR:(h + 1) * HR], v - (GP - 1) / 2.0)
 
         def coarse_a(v):
-            far = apool.tile([P, PASSES, NR, PACK, RUN], F32, tag="fara")
-            coarse(far[:], dist[:, 1], v)
+            far = apool.tile([P, PASSES, GA // GP, NRUNS[1], PACK, RUN], F32, tag="fara")
+            for j in range(GA // GP):
+                coarse(far[:, :, j], dist[1][:], v + j * GP - (GA - 1) / 2.0)
             return far
 
         def quad_gx(h, far, u):
@@ -123,7 +135,7 @@ def tile_gaussiansplatting_t_kernel(tc, positions, activities, position_scale, o
                     v = u * QUAD + j
                     nc.vector.tensor_tensor(
                         out=tiles[c][:, j * HG:(j + 2) * HG, :].rearrange("p (v r i) t -> p v r t i", v=2, i=RUN), in0=far[:, c, v:v + 2],
-                        in1=peak[:, 0, c, h * HR:(h + 1) * HR].unsqueeze(1).to_broadcast([P, 2, HR, PACK, RUN]), op=ALU.mult,
+                        in1=peak[0][:, c, h * HR:(h + 1) * HR].unsqueeze(1).to_broadcast([P, 2, HR, PACK, RUN]), op=ALU.mult,
                     )
             for c in range(PASSES):
                 cols = slice(h * HALF + u * QUAD * HG, h * HALF + (u + 1) * QUAD * HG)
@@ -136,7 +148,8 @@ def tile_gaussiansplatting_t_kernel(tc, positions, activities, position_scale, o
         def mult_a(v, c, far):
             grouped = gpool.tile([P, NGRP, PACK], BF16, tag="a", align_bytes=64)
             nc.vector.tensor_tensor(
-                out=grouped[:].rearrange("p (r i) t -> p r t i", i=RUN), in0=far[:, c], in1=peak[:, 1, c], op=ALU.mult,
+                out=grouped[:].rearrange("p (r i j) t -> p r t i j", i=RUN, j=GA // GP), in0=far[:, c].rearrange("p j r t i -> p r t i j"),
+                in1=peak[1][:, c].unsqueeze(4).to_broadcast([P, NRUNS[1], PACK, RUN, GA // GP]), op=ALU.mult,
             )
             a_grouped[v, c] = grouped
 
@@ -178,9 +191,9 @@ def tile_gaussiansplatting_t_kernel(tc, positions, activities, position_scale, o
         coarse_gx(far_x0, 0, 1, GP)
         distances(1, 0)
         distances(1, 1)
-        larger(peak[:, 0, 0], x0)
+        larger(peak[0][:, 0], x0)
         squares(1, 0)
-        larger(peak[:, 0, 1], x1)
+        larger(peak[0][:, 1], x1)
         squares(1, 1)
         y_pairs = [peak_exps(1, c) for c in range(PASSES)]
         far_a = [coarse_a(v) for v in range(GP // 2)]
@@ -190,15 +203,15 @@ def tile_gaussiansplatting_t_kernel(tc, positions, activities, position_scale, o
         quad_gx(0, far_x0, 0)
         best = []
         for c in range(PASSES):
-            b_tile = epool.tile([P, NR, PACK, RUN], F32, tag="best")
+            b_tile = epool.tile([P, NRUNS[1], PACK, RUN], F32, tag="best")
             best.append(b_tile)
         quad_gx(0, far_x0, 1)
         for c in range(PASSES):
             larger(best[c][:], y_pairs[c])
         for c in range(PASSES):
             nc.vector.tensor_tensor(
-                out=peak[:, 1, c], in0=best[c][:],
-                in1=act_sb[:, c, :].unsqueeze(1).unsqueeze(3).to_broadcast([P, NR, PACK, RUN]), op=ALU.mult,
+                out=peak[1][:, c], in0=best[c][:],
+                in1=act_sb[:, c, :].unsqueeze(1).unsqueeze(3).to_broadcast([P, NRUNS[1], PACK, RUN]), op=ALU.mult,
             )
 
         for v in range(GP // 2):

@@ -25,7 +25,7 @@ NR = NGRP // RUN
 NRUNS = (NR, RES // (GA * RUN))
 C_PIX = 1250.0 / (1023.0 * 1023.0)
 SHIFT = 0.125
-LIMIT = 8.0
+LIMIT = 4.0
 FLOPS = 2 * RES * RES * NPTS
 
 HALF = RES // 2
@@ -74,7 +74,6 @@ def tile_gaussiansplatting_t_kernel(tc, positions, activities, position_scale, o
         nc.vector.tensor_scalar(out=qs[:], in0=raw[:], scalar1=LIMIT, scalar2=-LIMIT, op0=ALU.min, op1=ALU.max)
         qn = const.tile([P, PASSES * PACK, 2], F32)
         nc.vector.tensor_scalar(out=qn[:, :, 0:1], in0=qs[:, :, 0:1], scalar1=-1024.0, scalar2=None, op0=ALU.mult)
-        nc.vector.tensor_scalar(out=qn[:, :, 1:2], in0=qs[:, :, 1:2], scalar1=1024.0, scalar2=None, op0=ALU.mult)
 
         dist, sq, peak = [], [], []
         for kind in range(2):
@@ -115,9 +114,9 @@ def tile_gaussiansplatting_t_kernel(tc, positions, activities, position_scale, o
         def coarse(out_ap, in_ap, step):
             nc.scalar.activation(out=out_ap, in_=in_ap, func=ACT.Exp, scale=-2.0 * C_PIX * step, bias=-C_PIX * step * step)
 
-        def coarse_gx(far, h, v0, v1):
+        def coarse_gx(far, h, v0, v1, passes=slice(0, PASSES)):
             for v in range(v0, v1):
-                coarse(far[:, :, v], dist[0][:, :, h * HR:(h + 1) * HR], v - (GP - 1) / 2.0)
+                coarse(far[:, passes, v], dist[0][:, passes, h * HR:(h + 1) * HR], v - (GP - 1) / 2.0)
 
         def coarse_a(v):
             far = apool.tile([P, PASSES, GA // GP, NRUNS[1], PACK, RUN], F32, tag="fara")
@@ -125,23 +124,33 @@ def tile_gaussiansplatting_t_kernel(tc, positions, activities, position_scale, o
                 coarse(far[:, :, j], dist[1][:], v + j * GP - (GA - 1) / 2.0)
             return far
 
+        quads = {}
+
+        def open_quad(h, u, c):
+            g_tile = gpool.tile([P, QUAD * HG, PACK], BF16, tag="gx", align_bytes=64)
+            quads[h, u, c] = g_tile
+
+        def mult_gx(h, far, u, c, j):
+            v = u * QUAD + j
+            nc.vector.tensor_tensor(
+                out=quads[h, u, c][:, j * HG:(j + 2) * HG, :].rearrange("p (v r i) t -> p v r t i", v=2, i=RUN), in0=far[:, c, v:v + 2],
+                in1=peak[0][:, c, h * HR:(h + 1) * HR].unsqueeze(1).to_broadcast([P, 2, HR, PACK, RUN]), op=ALU.mult,
+            )
+
+        def quant_gx(h, u, c):
+            cols = slice(h * HALF + u * QUAD * HG, h * HALF + (u + 1) * QUAD * HG)
+            nc.vector.quantize_mx(
+                out=gx_codes[:, c, cols].bitcast(FP8X4), scales=gx_scales[:, c, cols], in_=quads[h, u, c][:].rearrange("p w t -> p (w t)"),
+            )
+
         def quad_gx(h, far, u):
-            tiles = []
             for c in range(PASSES):
-                g_tile = gpool.tile([P, QUAD * HG, PACK], BF16, tag="gx", align_bytes=64)
-                tiles.append(g_tile)
+                open_quad(h, u, c)
             for j in range(0, QUAD, 2):
                 for c in range(PASSES):
-                    v = u * QUAD + j
-                    nc.vector.tensor_tensor(
-                        out=tiles[c][:, j * HG:(j + 2) * HG, :].rearrange("p (v r i) t -> p v r t i", v=2, i=RUN), in0=far[:, c, v:v + 2],
-                        in1=peak[0][:, c, h * HR:(h + 1) * HR].unsqueeze(1).to_broadcast([P, 2, HR, PACK, RUN]), op=ALU.mult,
-                    )
+                    mult_gx(h, far, u, c, j)
             for c in range(PASSES):
-                cols = slice(h * HALF + u * QUAD * HG, h * HALF + (u + 1) * QUAD * HG)
-                nc.vector.quantize_mx(
-                    out=gx_codes[:, c, cols].bitcast(FP8X4), scales=gx_scales[:, c, cols], in_=tiles[c][:].rearrange("p w t -> p (w t)"),
-                )
+                quant_gx(h, u, c)
 
         a_grouped = {}
 
@@ -176,22 +185,25 @@ def tile_gaussiansplatting_t_kernel(tc, positions, activities, position_scale, o
         out_rows = out.rearrange("(g v) w -> v g w", v=GP)
 
         def empty(v, h, copy):
-            stage = opool.tile([P, HR, RUN, GP], F32, tag="stage")
-            copy(out=stage[:].rearrange("p r i v -> p r v i"), in_=accs[v, h][:].rearrange("p v r i -> p r v i"))
-            nc.sync.dma_start(out=out_rows[v][:, h * HALF:(h + 1) * HALF], in_=stage[:].rearrange("p r i v -> p (r i v)"))
+            stage = opool.tile([P, HALF], F32, tag="stage")
+            copy(out=stage[:].rearrange("p (g v) -> p g v", v=GP), in_=accs[v, h][:].rearrange("p v r i -> p (r i) v"))
+            nc.sync.dma_start(out=out_rows[v][:, h * HALF:(h + 1) * HALF], in_=stage[:])
 
-        distances(0, 0)
-        distances(0, 1)
-        squares(0, 0)
-        squares(0, 1)
         far_x0 = xpool.tile([P, PASSES, GP, HR, PACK, RUN], F32, tag="farx")
-        coarse_gx(far_x0, 0, 0, 1)
+        distances(0, 0)
+        squares(0, 0)
+        nc.vector.tensor_scalar(out=qn[:, :, 1:2], in0=qs[:, :, 1:2], scalar1=1024.0, scalar2=None, op0=ALU.mult)
+        distances(0, 1)
+        squares(0, 1)
+        coarse_gx(far_x0, 0, 0, 1, slice(0, 1))
         x0 = peak_exps(0, 0)
         x1 = peak_exps(0, 1)
-        coarse_gx(far_x0, 0, 1, GP)
+        coarse_gx(far_x0, 0, 1, 2, slice(0, 1))
+        coarse_gx(far_x0, 0, 0, 2, slice(1, 2))
+        coarse_gx(far_x0, 0, 2, GP)
         distances(1, 0)
-        distances(1, 1)
         larger(peak[0][:, 0], x0)
+        distances(1, 1)
         squares(1, 0)
         larger(peak[0][:, 1], x1)
         squares(1, 1)

@@ -47,10 +47,10 @@ def tile_gaussiansplatting_t_kernel(tc, positions, activities, position_scale, o
         psum = ctx.enter_context(tc.psum_pool(name="psum", bufs=8))
         ctx.enter_context(tc.manual_schedule())
 
+        scl_sb = const.tile([P, 1], BF16)
+        nc.sync.dma_start(out=scl_sb[:], in_=position_scale.partition_broadcast(P))
         pos_sb = const.tile([P, PASSES, PACK * 2], BF16)
         nc.sync.dma_start(out=pos_sb[:], in_=positions.rearrange("(c p t) d -> p c (t d)", c=PASSES, p=P, t=PACK))
-        scl_sb = const.tile([P, 1], BF16)
-        nc.scalar.dma_start(out=scl_sb[:], in_=position_scale.partition_broadcast(P))
         act_sb = const.tile([P, PASSES, PACK], BF16)
         nc.sync.dma_start(out=act_sb[:], in_=activities.rearrange("(c p t) -> p c t", c=PASSES, p=P, t=PACK))
 
@@ -65,15 +65,22 @@ def tile_gaussiansplatting_t_kernel(tc, positions, activities, position_scale, o
             )
             centre.append(tab)
 
-        raw = const.tile([P, PASSES * PACK, 2], F32)
-        nc.vector.scalar_tensor_tensor(
-            out=raw[:].rearrange("p n d -> p (n d)"), in0=pos_sb[:].rearrange("p c n -> p (c n)"), scalar=-0.5,
-            in1=scl_sb[:].to_broadcast([P, PASSES * PACK * 2]), op0=ALU.add, op1=ALU.mult,
-        )
-        qs = const.tile([P, PASSES * PACK, 2], F32)
-        nc.vector.tensor_scalar(out=qs[:], in0=raw[:], scalar1=LIMIT, scalar2=-LIMIT, op0=ALU.min, op1=ALU.max)
-        qn = const.tile([P, PASSES * PACK, 2], F32)
-        nc.vector.tensor_scalar(out=qn[:, :, 0:1], in0=qs[:, :, 0:1], scalar1=-1024.0, scalar2=None, op0=ALU.mult)
+        scl_n = const.tile([P, 1], F32)
+        nc.vector.tensor_scalar(out=scl_n[:], in0=scl_sb[:], scalar1=-1024.0, scalar2=None, op0=ALU.mult)
+        coords = []
+        raws = []
+        for n, scl in enumerate((scl_sb, scl_n)):
+            raw = const.tile([P, PASSES * PACK, 2], F32, name="raw%d" % n)
+            nc.vector.scalar_tensor_tensor(
+                out=raw[:].rearrange("p n d -> p (n d)"), in0=pos_sb[:].rearrange("p c n -> p (c n)"), scalar=-0.5,
+                in1=scl[:].to_broadcast([P, PASSES * PACK * 2]), op0=ALU.add, op1=ALU.mult,
+            )
+            raws.append(raw)
+        for n, limit in enumerate((LIMIT, 1024.0 * LIMIT)):
+            kept = const.tile([P, PASSES * PACK, 2], F32, name="kept%d" % n)
+            nc.vector.tensor_scalar(out=kept[:], in0=raws[n][:], scalar1=limit, scalar2=-limit, op0=ALU.min, op1=ALU.max)
+            coords.append(kept)
+        qs, qn = coords
 
         dist, sq, peak = [], [], []
         for kind in range(2):
@@ -90,17 +97,17 @@ def tile_gaussiansplatting_t_kernel(tc, positions, activities, position_scale, o
                 n = c * PACK + t
                 nc.vector.tensor_scalar(
                     out=dist[kind][:, c, :, t, :], in0=centre[kind][:], scalar1=qn[:, n, kind:kind + 1], scalar2=qs[:, n, kind:kind + 1],
-                    op0=ALU.add, op1=ALU.add if kind == 0 else ALU.subtract,
+                    op0=ALU.add if kind == 0 else ALU.subtract, op1=ALU.add if kind == 0 else ALU.subtract,
                 )
 
-        def squares(kind, c):
-            nc.vector.tensor_tensor(out=sq[kind][:, c], in0=dist[kind][:, c], in1=dist[kind][:, c], op=ALU.mult)
+        def squares(kind, c0, c1):
+            nc.vector.tensor_tensor(out=sq[kind][:, c0:c1], in0=dist[kind][:, c0:c1], in1=dist[kind][:, c0:c1], op=ALU.mult)
 
-        def peak_exps(kind, c):
-            ea = epool.tile([P, NRUNS[kind], PACK, RUN], F32, tag="ea%d" % kind)
-            nc.scalar.activation(out=ea[:], in_=sq[kind][:, c], func=ACT.Exp, scale=-C_PIX)
-            eb = epool.tile([P, NRUNS[kind], PACK, RUN], F32, tag="eb%d" % kind)
-            nc.scalar.activation(out=eb[:], in_=sq[kind][:, c], func=ACT.Exp, scale=-C_PIX, bias=SHIFT)
+        def peak_exps(kind, c0, c1):
+            ea = epool.tile([P, c1 - c0, NRUNS[kind], PACK, RUN], F32, tag="ea%d" % kind)
+            nc.scalar.activation(out=ea[:], in_=sq[kind][:, c0:c1], func=ACT.Exp, scale=-C_PIX)
+            eb = epool.tile([P, c1 - c0, NRUNS[kind], PACK, RUN], F32, tag="eb%d" % kind)
+            nc.scalar.activation(out=eb[:], in_=sq[kind][:, c0:c1], func=ACT.Exp, scale=-C_PIX, bias=SHIFT)
             return ea, eb
 
         def larger(out_ap, pair):
@@ -191,38 +198,37 @@ def tile_gaussiansplatting_t_kernel(tc, positions, activities, position_scale, o
 
         far_x0 = xpool.tile([P, PASSES, GP, HR, PACK, RUN], F32, tag="farx")
         distances(0, 0)
-        squares(0, 0)
-        nc.vector.tensor_scalar(out=qn[:, :, 1:2], in0=qs[:, :, 1:2], scalar1=1024.0, scalar2=None, op0=ALU.mult)
         distances(0, 1)
-        squares(0, 1)
-        coarse_gx(far_x0, 0, 0, 1, slice(0, 1))
-        x0 = peak_exps(0, 0)
-        x1 = peak_exps(0, 1)
-        coarse_gx(far_x0, 0, 1, 2, slice(0, 1))
+        squares(0, 0, 1)
+        squares(0, 1, 2)
+        coarse_gx(far_x0, 0, 0, 2, slice(0, 1))
+        x0 = peak_exps(0, 0, 1)
+        x1 = peak_exps(0, 1, 2)
         coarse_gx(far_x0, 0, 0, 2, slice(1, 2))
         coarse_gx(far_x0, 0, 2, GP)
         distances(1, 0)
-        larger(peak[0][:, 0], x0)
         distances(1, 1)
-        squares(1, 0)
-        larger(peak[0][:, 1], x1)
-        squares(1, 1)
-        y_pairs = [peak_exps(1, c) for c in range(PASSES)]
+        squares(1, 0, PASSES)
+        larger(peak[0][:, 0:1], x0)
+        larger(peak[0][:, 1:2], x1)
+        y_pair = peak_exps(1, 0, PASSES)
         far_a = [coarse_a(v) for v in range(GP // 2)]
         far_x1 = xpool.tile([P, PASSES, GP, HR, PACK, RUN], F32, tag="farx")
         coarse_gx(far_x1, 1, 0, GP)
 
         quad_gx(0, far_x0, 0)
-        best = []
         for c in range(PASSES):
-            b_tile = epool.tile([P, NRUNS[1], PACK, RUN], F32, tag="best")
-            best.append(b_tile)
-        quad_gx(0, far_x0, 1)
+            open_quad(0, 1, c)
+        for j in range(0, QUAD, 2):
+            for c in range(PASSES):
+                mult_gx(0, far_x0, 1, c, j)
+        best = epool.tile([P, PASSES, NRUNS[1], PACK, RUN], F32, tag="best")
+        larger(best[:], y_pair)
         for c in range(PASSES):
-            larger(best[c][:], y_pairs[c])
+            quant_gx(0, 1, c)
         for c in range(PASSES):
             nc.vector.tensor_tensor(
-                out=peak[1][:, c], in0=best[c][:],
+                out=peak[1][:, c], in0=best[:, c],
                 in1=act_sb[:, c, :].unsqueeze(1).unsqueeze(3).to_broadcast([P, NRUNS[1], PACK, RUN]), op=ALU.mult,
             )
 

import math
from contextlib import ExitStack

import concourse.mybir as mybir

F32 = mybir.dt.float32
BF16 = mybir.dt.bfloat16
I32 = mybir.dt.int32
U32 = mybir.dt.uint32
U8 = mybir.dt.uint8
FP8X4 = mybir.dt.float8_e4m3fn_x4
ACT = mybir.ActivationFunctionType
ALU = mybir.AluOpType

P = 128
PACK = 4
RES = 1024
NPTS = 1024
PASSES = NPTS // (P * PACK)
GP = 8
GA = 16
NGRP = RES // GP
RUN = 4
NR = NGRP // RUN
NRUNS = (NR, RES // (GA * RUN))
C_PIX = 1250.0 / (1023.0 * 1023.0)
SHIFT = 0.125
LIMIT = 4.0
FLOPS = 2 * RES * RES * NPTS

HALF = RES // 2
HR = NR // 2
HG = NGRP // 2
QUAD = GP // 2


def tile_gaussiansplatting_t_kernel(tc, positions, activities, position_scale, out):
    nc = tc.nc
    with ExitStack() as ctx:
        const = ctx.enter_context(tc.tile_pool(name="const", bufs=1))
        keep = ctx.enter_context(tc.tile_pool(name="keep", bufs=1))
        epool = ctx.enter_context(tc.tile_pool(name="epool", bufs=4))
        xpool = ctx.enter_context(tc.tile_pool(name="xpool", bufs=2))
        apool = ctx.enter_context(tc.tile_pool(name="apool", bufs=8))
        gpool = ctx.enter_context(tc.tile_pool(name="gpool", bufs=4))
        opool = ctx.enter_context(tc.tile_pool(name="opool", bufs=16))
        psum = ctx.enter_context(tc.psum_pool(name="psum", bufs=8))
        ctx.enter_context(tc.manual_schedule())

        scl_sb = const.tile([P, 1], BF16)
        nc.sync.dma_start(out=scl_sb[:], in_=position_scale.partition_broadcast(P))
        pos_sb = const.tile([P, PASSES, PACK * 2], BF16)
        nc.sync.dma_start(out=pos_sb[:], in_=positions.rearrange("(c p t) d -> p c (t d)", c=PASSES, p=P, t=PACK))
        act_sb = const.tile([P, PASSES, PACK], BF16)
        nc.sync.dma_start(out=act_sb[:], in_=activities.rearrange("(c p t) -> p c t", c=PASSES, p=P, t=PACK))

        g_int = const.tile([P, NGRP], I32)
        nc.gpsimd.iota(g_int[:], pattern=[[1, NGRP]], base=0, channel_multiplier=0)
        centre = []
        for size in (GP, GA):
            tab = const.tile([P, RES // (size * RUN), RUN], F32, name="centre%d" % size)
            nc.vector.tensor_scalar(
                out=tab[:].rearrange("p r i -> p (r i)"), in0=g_int[:, 0:RES // size],
                scalar1=float(size), scalar2=(size - 1) / 2.0 - 511.5, op0=ALU.mult, op1=ALU.add,
            )
            centre.append(tab)

        scl_n = const.tile([P, 1], F32)
        nc.vector.tensor_scalar(out=scl_n[:], in0=scl_sb[:], scalar1=-1024.0, scalar2=None, op0=ALU.mult)
        coords = []
        raws = []
        for n, scl in enumerate((scl_sb, scl_n)):
            raw = const.tile([P, PASSES * PACK, 2], F32, name="raw%d" % n)
            nc.vector.scalar_tensor_tensor(
                out=raw[:].rearrange("p n d -> p (n d)"), in0=pos_sb[:].rearrange("p c n -> p (c n)"), scalar=-0.5,
                in1=scl[:].to_broadcast([P, PASSES * PACK * 2]), op0=ALU.add, op1=ALU.mult,
            )
            raws.append(raw)
        for n, limit in enumerate((LIMIT, 1024.0 * LIMIT)):
            kept = const.tile([P, PASSES * PACK, 2], F32, name="kept%d" % n)
            nc.vector.tensor_scalar(out=kept[:], in0=raws[n][:], scalar1=limit, scalar2=-limit, op0=ALU.min, op1=ALU.max)
            coords.append(kept)
        qs, qn = coords

        dist, sq, peak = [], [], []
        for kind in range(2):
            shape = [P, PASSES, NRUNS[kind], PACK, RUN]
            d_tile = const.tile(shape, F32, name="dist%d" % kind)
            dist.append(d_tile)
            s_tile = const.tile(shape, F32, name="sq%d" % kind)
            sq.append(s_tile)
            p_tile = const.tile(shape, F32, name="peak%d" % kind)
            peak.append(p_tile)

        def distances(kind, c):
            for t in range(PACK):
                n = c * PACK + t
                nc.vector.tensor_scalar(
                    out=dist[kind][:, c, :, t, :], in0=centre[kind][:], scalar1=qn[:, n, kind:kind + 1], scalar2=qs[:, n, kind:kind + 1],
                    op0=ALU.add if kind == 0 else ALU.subtract, op1=ALU.add if kind == 0 else ALU.subtract,
                )

        def squares(kind, c0, c1):
            nc.vector.tensor_tensor(out=sq[kind][:, c0:c1], in0=dist[kind][:, c0:c1], in1=dist[kind][:, c0:c1], op=ALU.mult)

        def peak_exps(kind, c0, c1):
            ea = epool.tile([P, c1 - c0, NRUNS[kind], PACK, RUN], F32, tag="ea%d" % kind)
            nc.scalar.activation(out=ea[:], in_=sq[kind][:, c0:c1], func=ACT.Exp, scale=-C_PIX)
            eb = epool.tile([P, c1 - c0, NRUNS[kind], PACK, RUN], F32, tag="eb%d" % kind)
            nc.scalar.activation(out=eb[:], in_=sq[kind][:, c0:c1], func=ACT.Exp, scale=-C_PIX, bias=SHIFT)
            return ea, eb

        def larger(out_ap, pair):
            nc.vector.scalar_tensor_tensor(out=out_ap, in0=pair[1][:], scalar=math.exp(-SHIFT), in1=pair[0][:], op0=ALU.mult, op1=ALU.max)

        gx_codes = keep.tile([P, PASSES, RES], U32, align_bytes=64)
        gx_scales = keep.tile([P, PASSES, RES], U8, align_bytes=64)
        a_codes = keep.tile([P, GP, PASSES, NGRP], U32, align_bytes=64)
        a_scales = keep.tile([P, GP, PASSES, NGRP], U8, align_bytes=64)

        def coarse(out_ap, in_ap, step):
            nc.scalar.activation(out=out_ap, in_=in_ap, func=ACT.Exp, scale=-2.0 * C_PIX * step, bias=-C_PIX * step * step)

        def coarse_gx(far, h, v0, v1, passes=slice(0, PASSES)):
            for v in range(v0, v1):
                coarse(far[:, passes, v], dist[0][:, passes, h * HR:(h + 1) * HR], v - (GP - 1) / 2.0)

        def coarse_a(v):
            far = apool.tile([P, PASSES, GA // GP, NRUNS[1], PACK, RUN], F32, tag="fara")
            for j in range(GA // GP):
                coarse(far[:, :, j], dist[1][:], v + j * GP - (GA - 1) / 2.0)
            return far

        quads = {}

        def open_quad(h, u, c):
            g_tile = gpool.tile([P, QUAD * HG, PACK], BF16, tag="gx", align_bytes=64)
            quads[h, u, c] = g_tile

        def mult_gx(h, far, u, c, j):
            v = u * QUAD + j
            nc.vector.tensor_tensor(
                out=quads[h, u, c][:, j * HG:(j + 2) * HG, :].rearrange("p (v r i) t -> p v r t i", v=2, i=RUN), in0=far[:, c, v:v + 2],
                in1=peak[0][:, c, h * HR:(h + 1) * HR].unsqueeze(1).to_broadcast([P, 2, HR, PACK, RUN]), op=ALU.mult,
            )

        def quant_gx(h, u, c):
            cols = slice(h * HALF + u * QUAD * HG, h * HALF + (u + 1) * QUAD * HG)
            nc.vector.quantize_mx(
                out=gx_codes[:, c, cols].bitcast(FP8X4), scales=gx_scales[:, c, cols], in_=quads[h, u, c][:].rearrange("p w t -> p (w t)"),
            )

        def quad_gx(h, far, u):
            for c in range(PASSES):
                open_quad(h, u, c)
            for j in range(0, QUAD, 2):
                for c in range(PASSES):
                    mult_gx(h, far, u, c, j)
            for c in range(PASSES):
                quant_gx(h, u, c)

        a_grouped = {}

        def mult_a(v, c, far):
            grouped = gpool.tile([P, NGRP, PACK], BF16, tag="a", align_bytes=64)
            nc.vector.tensor_tensor(
                out=grouped[:].rearrange("p (r i j) t -> p r t i j", i=RUN, j=GA // GP), in0=far[:, c].rearrange("p j r t i -> p r t i j"),
                in1=peak[1][:, c].unsqueeze(4).to_broadcast([P, NRUNS[1], PACK, RUN, GA // GP]), op=ALU.mult,
            )
            a_grouped[v, c] = grouped

        def quant_a(v, c):
            nc.vector.quantize_mx(
                out=a_codes[:, v, c].bitcast(FP8X4), scales=a_scales[:, v, c], in_=a_grouped[v, c][:].rearrange("p w t -> p (w t)"),
            )

        accs = {}

        def open_bank(v, h):
            acc = psum.tile([P, GP, HR, RUN], F32, tag="acc")
            accs[v, h] = acc

        def one_pass(v, h, c, v0=0, v1=GP):
            cols = slice(h * HALF + v0 * HG, h * HALF + v1 * HG)
            nc.tensor.matmul_mx(
                out=accs[v, h][:, v0:v1].rearrange("p v r i -> p (v r i)"),
                lhsT=a_codes[:, v, c].bitcast(FP8X4), lhsT_scale=a_scales[:, v, c],
                rhs=gx_codes[:, c, cols].bitcast(FP8X4), rhs_scale=gx_scales[:, c, cols],
                start=(c == 0), stop=(c == PASSES - 1),
            )

        out_rows = out.rearrange("(g v) w -> v g w", v=GP)

        def empty(v, h, copy):
            stage = opool.tile([P, HALF], F32, tag="stage")
            copy(out=stage[:].rearrange("p (g v) -> p g v", v=GP), in_=accs[v, h][:].rearrange("p v r i -> p (r i) v"))
            nc.sync.dma_start(out=out_rows[v][:, h * HALF:(h + 1) * HALF], in_=stage[:])

        far_x0 = xpool.tile([P, PASSES, GP, HR, PACK, RUN], F32, tag="farx")
        distances(0, 0)
        distances(0, 1)
        squares(0, 0, 1)
        squares(0, 1, 2)
        coarse_gx(far_x0, 0, 0, 2, slice(0, 1))
        x0 = peak_exps(0, 0, 1)
        x1 = peak_exps(0, 1, 2)
        coarse_gx(far_x0, 0, 0, 2, slice(1, 2))
        coarse_gx(far_x0, 0, 2, GP)
        distances(1, 0)
        distances(1, 1)
        squares(1, 0, PASSES)
        larger(peak[0][:, 0:1], x0)
        larger(peak[0][:, 1:2], x1)
        y_pair = peak_exps(1, 0, PASSES)
        far_a = [coarse_a(v) for v in range(GP // 2)]
        far_x1 = xpool.tile([P, PASSES, GP, HR, PACK, RUN], F32, tag="farx")
        coarse_gx(far_x1, 1, 0, GP)

        quad_gx(0, far_x0, 0)
        for c in range(PASSES):
            open_quad(0, 1, c)
        for j in range(0, QUAD, 2):
            for c in range(PASSES):
                mult_gx(0, far_x0, 1, c, j)
        best = epool.tile([P, PASSES, NRUNS[1], PACK, RUN], F32, tag="best")
        larger(best[:], y_pair)
        for c in range(PASSES):
            quant_gx(0, 1, c)
        for c in range(PASSES):
            nc.vector.tensor_tensor(
                out=peak[1][:, c], in0=best[:, c],
                in1=act_sb[:, c, :].unsqueeze(1).unsqueeze(3).to_broadcast([P, NRUNS[1], PACK, RUN]), op=ALU.mult,
            )

        for v in range(GP // 2):
            open_bank(v, 0)
            mult_a(v, 0, far_a[v])
            if v > 0:
                quant_a(v - 1, 1)
                one_pass(v - 1, 0, 1)
            mult_a(v, 1, far_a[v])
            quant_a(v, 0)
            one_pass(v, 0, 0)
        quant_a(GP // 2 - 1, 1)
        one_pass(GP // 2 - 1, 0, 1)

        for v in range(GP // 2):
            open_bank(v, 1)
        for u in range(GP // QUAD):
            quad_gx(1, far_x1, u)
            for v in range(GP // 2):
                for c in range(PASSES):
                    one_pass(v, 1, c, u * QUAD, (u + 1) * QUAD)
        for v in range(GP // 2):
            empty(v, 0, nc.scalar.copy)
        far_a += [coarse_a(v) for v in range(GP // 2, GP)]
        for v in range(GP // 2):
            empty(v, 1, nc.scalar.copy)

        for v in range(GP // 2, GP):
            for h in range(2):
                open_bank(v, h)
            mult_a(v, 0, far_a[v])
            if v > GP // 2:
                quant_a(v - 1, 1)
                for h in range(2):
                    one_pass(v - 1, h, 1)
                    empty(v - 1, h, nc.scalar.copy)
            if v < GP - 1:
                mult_a(v, 1, far_a[v])
                quant_a(v, 0)
            else:
                quant_a(v, 0)
                mult_a(v, 1, far_a[v])
            for h in range(2):
                one_pass(v, h, 0)
        v = GP - 1
        quant_a(v, 1)
        for h in range(2):
            one_pass(v, h, 1)
        empty(v, 0, nc.scalar.copy)
        empty(v, 1, nc.vector.tensor_copy)
